import numpy as np
import ml_dtypes


def mxq(x, axis, fmt="e4m3"):
    dtype, down = {"e4m3": (ml_dtypes.float8_e4m3fn, 7), "e5m2": (ml_dtypes.float8_e5m2, 14)}[fmt]
    v = np.moveaxis(np.asarray(x, np.float32).astype(ml_dtypes.bfloat16).astype(np.float64), axis, -1)
    blocks = v.reshape(v.shape[:-1] + (-1, 32))
    amax = np.abs(blocks).max(-1, keepdims=True)
    byte = np.maximum(np.where(amax > 0, np.frexp(amax)[1] - 1 + 127, 0) - down, 1)
    scale = np.exp2(byte - 127.0)
    codes = (blocks / scale).astype(np.float32).astype(dtype).astype(np.float64)
    return np.moveaxis((codes * scale).reshape(v.shape), -1, axis)


WIDE = False


def mx_kscale(k):
    if not WIDE:
        return np.ones(k)
    levels = np.array([10, -10, 5, -5, 0])
    a = np.random.permutation(np.resize(levels, k // 512 * 4)).reshape(k // 512, 4)
    idx = np.arange(k)
    return np.exp2(a[idx // 512, idx % 128 // 32])


BF16 = ml_dtypes.bfloat16


def bf(x):
    return np.asarray(x, np.float32).astype(BF16)


def f64(x):
    return np.asarray(x).astype(np.float64)


E2M1 = np.array([0.0, 0.5, 1.0, 1.5, 2.0, 3.0, 4.0, 6.0, -0.0, -0.5, -1.0, -1.5, -2.0, -3.0, -4.0, -6.0])


def pack_weight(w, fmt):
    k, n = w.shape
    w = f64(bf(w)).reshape(k // 32, 32, n)
    amax = np.abs(w).max(1)
    if fmt == "e4m3":
        byte = np.frexp(amax)[1] - 1 + 127 - 7
    else:
        mant, ex = np.frexp(amax / 6.0)
        byte = np.where(mant > 0.5, ex, ex - 1) + 127
    byte = np.clip(np.where(amax > 0, byte, 1), 1, 254)
    scaled = (w * np.exp2(127.0 - byte)[:, None, :]).reshape(k, n).astype(np.float32)
    by_word = np.ascontiguousarray(scaled.reshape(k // 512, 128, 4, n).transpose(0, 1, 3, 2))
    if fmt == "e4m3":
        words = by_word.astype(ml_dtypes.float8_e4m3fn).view(np.uint8)
    else:
        c = by_word.astype(ml_dtypes.float4_e2m1fn).view(np.uint8) & 0xF
        words = c[..., 0::2] | (c[..., 1::2] << 4)
    return np.ascontiguousarray(words), np.ascontiguousarray(byte.astype(np.uint8).reshape(k // 512, 16, n))


def unpack_weight(words, scales, fmt):
    g, p, n, _ = words.shape
    if fmt == "e4m3":
        vals = np.ascontiguousarray(words).view(ml_dtypes.float8_e4m3fn).astype(np.float64)
    else:
        nib = np.empty((g, p, n, 4), np.uint8)
        nib[..., 0::2] = words & 0xF
        nib[..., 1::2] = words >> 4
        vals = E2M1[nib]
    vals = vals * np.repeat(np.exp2(scales.astype(np.float64) - 127.0), 8, axis=1)[..., None]
    return vals.transpose(0, 1, 3, 2).reshape(g * 512, n)


B, STOCH, ACT_DIM, HIDDEN, DETER = 4096, 1024, 512, 2048, 512
EPS = 1e-4
DT_MIN = 1e-4
FMT = "e4m3"


def softplus(v):
    return np.maximum(v, 0.0) + np.log1p(np.exp(-np.abs(v)))


def sigmoid(v):
    return 1.0 / (1.0 + np.exp(-v))


def rmsnorm(v, w):
    return v * (1.0 / np.sqrt(np.mean(v * v, axis=-1, keepdims=True) + EPS)) * w


def setup_inputs():
    s = mx_kscale(DETER)
    r = np.maximum(s, 1.0)

    def w():
        return np.random.standard_normal((DETER, DETER)) / np.sqrt(DETER) / s

    def bias():
        return np.random.standard_normal(DETER) * 0.2

    x = bf(np.random.standard_normal((B, DETER)) * 0.9 * s)
    deter = bf(np.random.standard_normal((B, DETER)))
    a_base = bf(np.random.standard_normal(DETER))
    dt_w_words, dt_w_scales = pack_weight(np.ascontiguousarray(w().T), FMT)
    dt_b = bf(bias())
    b_w_words, b_w_scales = pack_weight(np.ascontiguousarray(w().T), FMT)
    b_b = bf(bias())
    c_w_words, c_w_scales = pack_weight(np.ascontiguousarray((w() / r[:, None]).T), FMT)
    c_b = bf(bias() / r)
    z_w_words, z_w_scales = pack_weight(np.ascontiguousarray(w().T), FMT)
    z_b = bf(bias())
    skip = bf(np.random.standard_normal(DETER) * 0.5 / s)
    norm_w = bf(1.0 + 0.1 * np.random.standard_normal(DETER))
    return {"x": x,
            "deter": deter,
            "a_base": a_base,
            "dt_w_words": dt_w_words, "dt_w_scales": dt_w_scales, "dt_b": dt_b,
            "b_w_words": b_w_words, "b_w_scales": b_w_scales, "b_b": b_b,
            "c_w_words": c_w_words, "c_w_scales": c_w_scales, "c_b": c_b,
            "z_w_words": z_w_words, "z_w_scales": z_w_scales, "z_b": z_b,
            "skip": skip,
            "norm_w": norm_w}


def reference(x, deter, a_base, dt_w_words, dt_w_scales, dt_b, b_w_words, b_w_scales, b_b, c_w_words, c_w_scales, c_b, z_w_words, z_w_scales, z_b, skip, norm_w):
    x, deter = f64(x), f64(deter)
    xq = mxq(x, 1, "e4m3")
    dt = softplus((xq @ unpack_weight(dt_w_words, dt_w_scales, FMT)) + f64(dt_b)) + DT_MIN
    a = -softplus(f64(a_base))
    b = np.tanh((xq @ unpack_weight(b_w_words, b_w_scales, FMT)) + f64(b_b))
    c = (xq @ unpack_weight(c_w_words, c_w_scales, FMT)) + f64(c_b)
    z = sigmoid((xq @ unpack_weight(z_w_words, z_w_scales, FMT)) + f64(z_b))
    state = np.exp(a * dt) * deter + dt * b * x
    y = c * state + f64(skip) * x
    out = z * y + (1.0 - z) * deter
    return rmsnorm(out, f64(norm_w))

@@ -1,0 +1,357 @@
+from contextlib import ExitStack
+
+import concourse.mybir as mybir
+from concourse.masks import make_identity
+
+F32 = mybir.dt.float32
+BF16 = mybir.dt.bfloat16
+I32 = mybir.dt.int32
+U32 = mybir.dt.uint32
+U8 = mybir.dt.uint8
+FP8X4 = mybir.dt.float8_e4m3fn_x4
+ALU = mybir.AluOpType
+FUNC = mybir.ActivationFunctionType
+
+P = 128
+TOKENS = 4096
+CHANNELS = 512
+BLOCKS = CHANNELS // P
+TILES = TOKENS // P
+TILES_PER_CHUNK = 4
+CHUNK = TILES_PER_CHUNK * P
+CHUNKS = TOKENS // CHUNK
+WORDS = CHANNELS // 2
+
+DT_MIN = 1e-4
+EPS = 1e-4
+SOFTPLUS_FLOOR = -40.0
+
+W_DT, W_B, W_C, W_Z = 0, 1, 2, 3
+V_DT_B, V_B_B, V_C_B, V_Z_B, V_A_BASE, V_SKIP = 0, 1, 2, 3, 4, 5
+VECTORS = 6
+
+FLOPS = 2 * TOKENS * CHANNELS * CHANNELS * 4
+
+
+def tile_mamba2backbone_pb_t_kernel(
+    tc,
+    x,
+    deter,
+    a_base,
+    dt_w_words,
+    dt_w_scales,
+    dt_b,
+    b_w_words,
+    b_w_scales,
+    b_b,
+    c_w_words,
+    c_w_scales,
+    c_b,
+    z_w_words,
+    z_w_scales,
+    z_b,
+    skip,
+    norm_w,
+    out,
+):
+    nc = tc.nc
+    with ExitStack() as ctx:
+        ctx.enter_context(tc.manual_schedule())
+        keep = ctx.enter_context(tc.tile_pool(name="keep", bufs=1))
+        stage = ctx.enter_context(tc.tile_pool(name="stage", bufs=2))
+        work = ctx.enter_context(tc.tile_pool(name="work", bufs=2))
+        rows = ctx.enter_context(tc.tile_pool(name="rows", bufs=3))
+        psum_scalar = ctx.enter_context(tc.psum_pool(name="psum_scalar", bufs=2))
+        psum_vector = ctx.enter_context(tc.psum_pool(name="psum_vector", bufs=2))
+        psum_turned = ctx.enter_context(tc.psum_pool(name="psum_turned", bufs=2))
+        psum_back = ctx.enter_context(tc.psum_pool(name="psum_back", bufs=2))
+
+        x_rows = x.rearrange("(p n) c -> p n c", n=TILES)
+        deter_rows = deter.rearrange("(p n) c -> p n c", n=TILES)
+        out_rows = out.rearrange("(p n) c -> p n c", n=TILES)
+
+        x_sb = keep.tile([P, TILES, CHANNELS], BF16)
+        deter_sb = keep.tile([P, TILES, CHANNELS], BF16)
+        w_codes = keep.tile([P, 4, CHANNELS], U32, align_bytes=64)
+        w_planes = keep.tile([P, 4, CHANNELS], U8, align_bytes=64)
+        x_codes = keep.tile([P, CHUNKS, CHUNK], U32, align_bytes=64)
+        x_planes = keep.tile([P, CHUNKS, CHUNK], U8, align_bytes=64)
+        vector_rows = keep.tile([P, P], BF16)
+        norm_w_all = keep.tile([P, CHANNELS], BF16)
+        ident_bf16 = keep.tile([P, P], BF16)
+        ident_f32 = keep.tile([P, P], F32)
+
+        def chunk_tiles(c):
+            return slice(c * TILES_PER_CHUNK, (c + 1) * TILES_PER_CHUNK)
+
+        def block(j):
+            return slice(j * P, (j + 1) * P)
+
+        def load_weight(w, words, scales):
+            for quadrant in range(4):
+                nc.sync.dma_start(
+                    out=w_planes[32 * quadrant : 32 * quadrant + 4, w, :].bitcast(I32),
+                    in_=scales[0, 4 * quadrant : 4 * quadrant + 4, :].bitcast(I32),
+                )
+            nc.sync.dma_start(
+                out=w_codes[:, w, :].bitcast(I32),
+                in_=words[0].rearrange("p n t -> p (n t)").bitcast(I32),
+            )
+
+        nc.vector.memset(w_planes[:].rearrange("p w n -> p (w n)").bitcast(I32), 0)
+        nc.vector.memset(vector_rows[:], 0.0)
+        nc.sync.dma_start(out=x_sb[:, chunk_tiles(0), :], in_=x_rows[:, chunk_tiles(0), :])
+        for v, vector in enumerate((dt_b, b_b, c_b, z_b, a_base, skip)):
+            nc.scalar.dma_start(
+                out=vector_rows[BLOCKS * v : BLOCKS * (v + 1), :],
+                in_=vector.rearrange("(j p) -> j p", p=P),
+            )
+        load_weight(W_DT, dt_w_words, dt_w_scales)
+        load_weight(W_B, b_w_words, b_w_scales)
+        load_weight(W_Z, z_w_words, z_w_scales)
+        nc.sync.dma_start(out=x_sb[:, chunk_tiles(1), :], in_=x_rows[:, chunk_tiles(1), :])
+        load_weight(W_C, c_w_words, c_w_scales)
+        nc.scalar.dma_start(out=norm_w_all[:], in_=norm_w.partition_broadcast(P))
+        for c in range(CHUNKS):
+            nc.sync.dma_start(
+                out=deter_sb[:, chunk_tiles(c), :], in_=deter_rows[:, chunk_tiles(c), :]
+            )
+            if c + 2 < CHUNKS:
+                nc.sync.dma_start(
+                    out=x_sb[:, chunk_tiles(c + 2), :], in_=x_rows[:, chunk_tiles(c + 2), :]
+                )
+
+        make_identity(nc, ident_f32[:])
+        make_identity(nc, ident_bf16[:])
+        one_col = keep.tile([P, 1], F32)
+        dt_min_col = keep.tile([P, 1], F32)
+        eps_col = keep.tile([P, 1], F32)
+        nc.vector.memset(one_col[:], 1.0)
+        nc.vector.memset(dt_min_col[:], DT_MIN)
+        nc.vector.memset(eps_col[:], EPS)
+
+        params = keep.tile([P, VECTORS, BLOCKS], F32)
+        dt_b_shifted = keep.tile([P, BLOCKS], F32)
+        z_b_half = keep.tile([P, BLOCKS], F32)
+        a_floor = keep.tile([P, BLOCKS], F32)
+        a_exp = keep.tile([P, BLOCKS], F32)
+        a_neg = keep.tile([P, BLOCKS], F32)
+
+        def prepare_parameters():
+            turned = psum_scalar.tile([P, P], BF16, tag="scalar")
+            nc.tensor.transpose(turned[:], vector_rows[:], ident_bf16[:])
+            nc.vector.tensor_copy(
+                out=params[:].rearrange("p v j -> p (v j)"), in_=turned[:, 0 : VECTORS * BLOCKS]
+            )
+            nc.vector.tensor_scalar_add(out=dt_b_shifted[:], in0=params[:, V_DT_B, :], scalar1=DT_MIN)
+            nc.vector.tensor_scalar_mul(out=z_b_half[:], in0=params[:, V_Z_B, :], scalar1=0.5)
+            nc.vector.tensor_scalar_max(out=a_floor[:], in0=params[:, V_A_BASE, :], scalar1=SOFTPLUS_FLOOR)
+
+        grouped_of = {}
+        dt_of = {}
+        log_of = {}
+        b_of = {}
+        gate_of = {}
+        decay_of = {}
+        o_of = {}
+        sumsq_of = {}
+        rstd_of = {}
+
+        def live(c):
+            return 0 <= c < CHUNKS
+
+        def project(pool, tag, w, c, j):
+            acc = pool.tile([P, CHUNK], F32, tag=tag)
+            nc.tensor.matmul_mx(
+                out=acc[:],
+                lhsT=w_codes[:, w, block(j)].bitcast(FP8X4),
+                lhsT_scale=w_planes[:, w, block(j)],
+                rhs=x_codes[:, c, :].bitcast(FP8X4),
+                rhs_scale=x_planes[:, c, :],
+                start=True,
+                stop=True,
+            )
+            return acc
+
+        def turn_x_for_quantising(c):
+            grouped = stage.tile([P, CHUNK, 4], BF16, tag="grouped", align_bytes=64)
+            grouped_of[c] = grouped
+            grouped_words = (
+                grouped[:]
+                .rearrange("p r t -> p (r t)")
+                .bitcast(F32)
+                .rearrange("p (n r u) -> p n r u", n=TILES_PER_CHUNK, r=P, u=2)
+            )
+            for half in range(2):
+                turned = psum_scalar.tile([P, 2, 2, P], F32, tag="scalar")
+                for m in range(2):
+                    words = x_sb[:, c * TILES_PER_CHUNK + 2 * half + m, :].bitcast(F32)
+                    for u in range(2):
+                        nc.tensor.transpose(turned[:, m, u, :], words[:, u:WORDS:2], ident_f32[:])
+                nc.scalar.copy(
+                    out=grouped_words[:, 2 * half : 2 * half + 2, :, :],
+                    in_=turned[:].rearrange("p m u r -> p m r u"),
+                )
+
+        def quantise_x(c):
+            nc.vector.quantize_mx(
+                out=x_codes[:, c, :].bitcast(FP8X4),
+                scales=x_planes[:, c, :],
+                in_=grouped_of[c][:].rearrange("p r t -> p (r t)"),
+            )
+
+        def floor_dt_input(c):
+            dt = work.tile([P, BLOCKS, CHUNK], F32, tag="dt")
+            dt_of[c] = dt
+            for j in range(BLOCKS):
+                acc = project(psum_vector, "vector", W_DT, c, j)
+                nc.vector.tensor_scalar(
+                    out=dt[:, j, :],
+                    in0=acc[:],
+                    scalar1=dt_b_shifted[:, j : j + 1],
+                    scalar2=SOFTPLUS_FLOOR,
+                    op0=ALU.add,
+                    op1=ALU.max,
+                )
+
+        def exp_and_tanh(c, j):
+            nc.scalar.activation(
+                out=log_of[c][:, j, :], in_=dt_of[c][:, j, :], func=FUNC.Exp, scale=-1.0, bias=dt_min_col[:]
+            )
+            acc_b = project(psum_scalar, "scalar", W_B, c, j)
+            nc.scalar.activation(
+                out=b_of[c][:, j, :], in_=acc_b[:], func=FUNC.Tanh, bias=params[:, V_B_B, j : j + 1]
+            )
+            acc_z = project(psum_scalar, "scalar", W_Z, c, j)
+            nc.scalar.activation(
+                out=gate_of[c][:, j, :], in_=acc_z[:], func=FUNC.Tanh, scale=0.5, bias=z_b_half[:, j : j + 1]
+            )
+
+        def finish_dt(c):
+            dt, log, b = dt_of[c], log_of[c], b_of[c]
+            decay = work.tile([P, BLOCKS, CHUNK], F32, tag="decay")
+            decay_of[c] = decay
+            for j in range(BLOCKS):
+                nc.gpsimd.tensor_tensor(out=dt[:, j, :], in0=dt[:, j, :], in1=log[:, j, :], op=ALU.add)
+            for j in range(BLOCKS):
+                nc.scalar.activation(
+                    out=decay[:, j, :], in_=dt[:, j, :], func=FUNC.Exp, scale=a_neg[:, j : j + 1]
+                )
+            for j in range(BLOCKS):
+                nc.gpsimd.tensor_tensor(out=b[:, j, :], in0=dt[:, j, :], in1=b[:, j, :], op=ALU.mult)
+
+        def state_terms(c, j):
+            deter_term, x_term = decay_of[c][:, j, :], b_of[c][:, j, :]
+            acc_c = project(psum_vector, "vector", W_C, c, j)
+            turned = psum_turned.tile([P, 2, CHUNK], BF16, tag="turned")
+            for side, source in enumerate((x_sb, deter_sb)):
+                for t in range(TILES_PER_CHUNK):
+                    nc.tensor.transpose(
+                        turned[:, side, block(t)],
+                        source[:, c * TILES_PER_CHUNK + t, block(j)],
+                        ident_bf16[:],
+                    )
+            c_bias = params[:, V_C_B, j : j + 1]
+            nc.vector.scalar_tensor_tensor(
+                out=deter_term, in0=acc_c[:], scalar=c_bias, in1=deter_term, op0=ALU.add, op1=ALU.mult
+            )
+            nc.vector.scalar_tensor_tensor(
+                out=deter_term, in0=deter_term, scalar=-1.0, in1=turned[:, 1, :], op0=ALU.add, op1=ALU.mult
+            )
+            nc.vector.scalar_tensor_tensor(
+                out=x_term, in0=acc_c[:], scalar=c_bias, in1=x_term, op0=ALU.add, op1=ALU.mult
+            )
+            nc.vector.scalar_tensor_tensor(
+                out=x_term,
+                in0=x_term,
+                scalar=params[:, V_SKIP, j : j + 1],
+                in1=turned[:, 0, :],
+                op0=ALU.add,
+                op1=ALU.mult,
+            )
+            nc.gpsimd.tensor_tensor(out=deter_term, in0=deter_term, in1=x_term, op=ALU.add)
+
+        def apply_gate(c, j):
+            gate = gate_of[c][:, j, :]
+            nc.vector.scalar_tensor_tensor(
+                out=gate, in0=gate, scalar=1.0, in1=decay_of[c][:, j, :], op0=ALU.add, op1=ALU.mult
+            )
+
+        def back_to_token_rows(c):
+            o = rows.tile([P, TILES_PER_CHUNK, CHANNELS], F32, tag="o")
+            sumsq = rows.tile([P, TILES_PER_CHUNK], F32, tag="sumsq")
+            o_of[c], sumsq_of[c] = o, sumsq
+            for t in range(TILES_PER_CHUNK):
+                back = psum_back.tile([P, CHANNELS], F32, tag="back")
+                for j in range(BLOCKS):
+                    nc.tensor.transpose(back[:, block(j)], gate_of[c][:, j, block(t)], ident_f32[:])
+                nc.vector.scalar_tensor_tensor(
+                    out=o[:, t, :],
+                    in0=back[:],
+                    scalar=0.5,
+                    in1=deter_sb[:, c * TILES_PER_CHUNK + t, :],
+                    op0=ALU.mult,
+                    op1=ALU.add,
+                )
+                squares = stage.tile([P, CHANNELS], BF16, tag="squares")
+                nc.scalar.activation(
+                    out=squares[:], in_=o[:, t, :], func=FUNC.Square, accum_out=sumsq[:, t : t + 1]
+                )
+
+        def normalise(c, t):
+            o = o_of[c][:, t, :]
+            nc.vector.scalar_tensor_tensor(
+                out=o, in0=o, scalar=rstd_of[c][:, t : t + 1], in1=norm_w_all[:], op0=ALU.mult, op1=ALU.mult
+            )
+
+        FIRST_PASS = -2
+        for i in range(FIRST_PASS, CHUNKS + 2):
+            if i == FIRST_PASS + 1:
+                prepare_parameters()
+            if live(i - 2):
+                rstd = rows.tile([P, TILES_PER_CHUNK], F32, tag="rstd")
+                rstd_of[i - 2] = rstd
+                nc.scalar.activation(out=rstd[:], in_=sumsq_of[i - 2][:], func=FUNC.Exp, scale=-0.5)
+            if live(i):
+                finish_dt(i)
+            if live(i + 1):
+                quantise_x(i + 1)
+            if live(i - 1):
+                back_to_token_rows(i - 1)
+            if live(i + 1):
+                floor_dt_input(i + 1)
+                log_next = work.tile([P, BLOCKS, CHUNK], F32, tag="log")
+                b_next = work.tile([P, BLOCKS, CHUNK], F32, tag="b")
+                gate_next = work.tile([P, BLOCKS, CHUNK], F32, tag="gate")
+                log_of[i + 1], b_of[i + 1], gate_of[i + 1] = log_next, b_next, gate_next
+            if live(i + 2):
+                turn_x_for_quantising(i + 2)
+            for j in range(BLOCKS):
+                if live(i):
+                    state_terms(i, j)
+                    if j > 0:
+                        apply_gate(i, j - 1)
+                if live(i + 1):
+                    exp_and_tanh(i + 1, j)
+            for t in range(TILES_PER_CHUNK):
+                if t == TILES_PER_CHUNK // 2 and live(i):
+                    apply_gate(i, BLOCKS - 1)
+                if live(i - 2):
+                    normalise(i - 2, t)
+            if live(i - 2):
+                nc.sync.dma_start(out=out_rows[:, chunk_tiles(i - 2), :], in_=o_of[i - 2][:])
+            if i == FIRST_PASS + 1:
+                nc.scalar.activation(out=a_exp[:], in_=a_floor[:], func=FUNC.Exp, scale=-1.0)
+                nc.scalar.activation(out=a_exp[:], in_=a_exp[:], func=FUNC.Ln, bias=one_col[:])
+                nc.vector.scalar_tensor_tensor(
+                    out=a_neg[:], in0=a_floor[:], scalar=-1.0, in1=a_exp[:], op0=ALU.mult, op1=ALU.subtract
+                )
+            if live(i + 1):
+                for j in range(BLOCKS):
+                    log = log_of[i + 1][:, j, :]
+                    nc.scalar.activation(out=log, in_=log, func=FUNC.Ln, bias=one_col[:])
+            if live(i - 1):
+                sumsq = sumsq_of[i - 1]
+                nc.scalar.activation(
+                    out=sumsq[:], in_=sumsq[:], func=FUNC.Ln, scale=1.0 / CHANNELS, bias=eps_col[:]
+                )

@@ -17,9 +17,11 @@ TOKENS = 4096
 CHANNELS = 512
 BLOCKS = CHANNELS // P
 TILES = TOKENS // P
-TILES_PER_CHUNK = 4
-CHUNK = TILES_PER_CHUNK * P
+CHUNK = 512
 CHUNKS = TOKENS // CHUNK
+QUARTERS = CHUNK // P
+assert QUARTERS == BLOCKS
+UNITS = CHUNKS * QUARTERS
 WORDS = CHANNELS // 2
 
 DT_MIN = 1e-4
@@ -30,7 +32,28 @@ W_DT, W_B, W_C, W_Z = 0, 1, 2, 3
 V_DT_B, V_B_B, V_C_B, V_Z_B, V_A_BASE, V_SKIP = 0, 1, 2, 3, 4, 5
 VECTORS = 6
 
+LAG_TURN_X = -6
+LAG_QUANTISE = -5
+LAG_FLOOR = -1
+LAG_EXP = 0
+LAG_TANH_B = 3
+LAG_DT = 4
+LAG_DECAY = 5
+LAG_TERMS = 6
+LAG_SUM = 7
+LAG_TANH_Z = 7
+LAG_GATE = 8
+LAG_BACK = 12
+LAG_NORM = 13
+assert LAG_FLOOR - LAG_QUANTISE >= QUARTERS
+assert LAG_DT - LAG_EXP >= BLOCKS
+assert LAG_BACK - LAG_GATE >= BLOCKS
+
 FLOPS = 2 * TOKENS * CHANNELS * CHANNELS * 4
+
+
+def slots(first_lag, last_lag):
+    return last_lag - first_lag + 2
 
 
 def tile_mamba2backbone_pb_t_kernel(
@@ -58,12 +81,11 @@ def tile_mamba2backbone_pb_t_kernel(
     with ExitStack() as ctx:
         ctx.enter_context(tc.manual_schedule())
         keep = ctx.enter_context(tc.tile_pool(name="keep", bufs=1))
-        stage = ctx.enter_context(tc.tile_pool(name="stage", bufs=2))
         work = ctx.enter_context(tc.tile_pool(name="work", bufs=2))
-        rows = ctx.enter_context(tc.tile_pool(name="rows", bufs=3))
         psum_scalar = ctx.enter_context(tc.psum_pool(name="psum_scalar", bufs=2))
         psum_vector = ctx.enter_context(tc.psum_pool(name="psum_vector", bufs=2))
-        psum_turned = ctx.enter_context(tc.psum_pool(name="psum_turned", bufs=2))
+        psum_words = ctx.enter_context(tc.psum_pool(name="psum_words", bufs=1))
+        psum_turned = ctx.enter_context(tc.psum_pool(name="psum_turned", bufs=1))
         psum_back = ctx.enter_context(tc.psum_pool(name="psum_back", bufs=2))
 
         x_rows = x.rearrange("(p n) c -> p n c", n=TILES)
@@ -79,13 +101,15 @@ def tile_mamba2backbone_pb_t_kernel(
         vector_rows = keep.tile([P, P], BF16)
         norm_w_all = keep.tile([P, CHANNELS], BF16)
         ident_bf16 = keep.tile([P, P], BF16)
+        twice_ident = keep.tile([P, P], BF16)
         ident_f32 = keep.tile([P, P], F32)
-
-        def chunk_tiles(c):
-            return slice(c * TILES_PER_CHUNK, (c + 1) * TILES_PER_CHUNK)
 
         def block(j):
             return slice(j * P, (j + 1) * P)
+
+        def load_rows(dst, src, c):
+            tiles = slice(c * QUARTERS, (c + 1) * QUARTERS)
+            nc.sync.dma_start(out=dst[:, tiles, :], in_=src[:, tiles, :])
 
         def load_weight(w, words, scales):
             for quadrant in range(4):
@@ -100,65 +124,68 @@ def tile_mamba2backbone_pb_t_kernel(
 
         nc.vector.memset(w_planes[:].rearrange("p w n -> p (w n)").bitcast(I32), 0)
         nc.vector.memset(vector_rows[:], 0.0)
-        nc.sync.dma_start(out=x_sb[:, chunk_tiles(0), :], in_=x_rows[:, chunk_tiles(0), :])
+        load_rows(x_sb, x_rows, 0)
         for v, vector in enumerate((dt_b, b_b, c_b, z_b, a_base, skip)):
             nc.scalar.dma_start(
                 out=vector_rows[BLOCKS * v : BLOCKS * (v + 1), :],
                 in_=vector.rearrange("(j p) -> j p", p=P),
             )
-        load_weight(W_DT, dt_w_words, dt_w_scales)
-        load_weight(W_B, b_w_words, b_w_scales)
-        load_weight(W_Z, z_w_words, z_w_scales)
-        nc.sync.dma_start(out=x_sb[:, chunk_tiles(1), :], in_=x_rows[:, chunk_tiles(1), :])
-        load_weight(W_C, c_w_words, c_w_scales)
         nc.scalar.dma_start(out=norm_w_all[:], in_=norm_w.partition_broadcast(P))
+        load_weight(W_DT, dt_w_words, dt_w_scales)
+        load_rows(x_sb, x_rows, 1)
+        load_weight(W_B, b_w_words, b_w_scales)
+        load_rows(x_sb, x_rows, 2)
+        load_weight(W_C, c_w_words, c_w_scales)
+        load_weight(W_Z, z_w_words, z_w_scales)
         for c in range(CHUNKS):
-            nc.sync.dma_start(
-                out=deter_sb[:, chunk_tiles(c), :], in_=deter_rows[:, chunk_tiles(c), :]
-            )
-            if c + 2 < CHUNKS:
-                nc.sync.dma_start(
-                    out=x_sb[:, chunk_tiles(c + 2), :], in_=x_rows[:, chunk_tiles(c + 2), :]
-                )
+            load_rows(deter_sb, deter_rows, c)
+            if c + 3 < CHUNKS:
+                load_rows(x_sb, x_rows, c + 3)
 
         make_identity(nc, ident_f32[:])
         make_identity(nc, ident_bf16[:])
+        nc.vector.tensor_scalar_mul(out=twice_ident[:], in0=ident_bf16[:], scalar1=2.0)
         one_col = keep.tile([P, 1], F32)
         dt_min_col = keep.tile([P, 1], F32)
-        eps_col = keep.tile([P, 1], F32)
+        minus_half_col = keep.tile([P, 1], F32)
         nc.vector.memset(one_col[:], 1.0)
         nc.vector.memset(dt_min_col[:], DT_MIN)
-        nc.vector.memset(eps_col[:], EPS)
+        nc.vector.memset(minus_half_col[:], -0.5)
 
         params = keep.tile([P, VECTORS, BLOCKS], F32)
         dt_b_shifted = keep.tile([P, BLOCKS], F32)
         z_b_half = keep.tile([P, BLOCKS], F32)
         a_floor = keep.tile([P, BLOCKS], F32)
-        a_exp = keep.tile([P, BLOCKS], F32)
+        a_log = keep.tile([P, BLOCKS], F32)
         a_neg = keep.tile([P, BLOCKS], F32)
 
-        def prepare_parameters():
-            turned = psum_scalar.tile([P, P], BF16, tag="scalar")
-            nc.tensor.transpose(turned[:], vector_rows[:], ident_bf16[:])
-            nc.vector.tensor_copy(
-                out=params[:].rearrange("p v j -> p (v j)"), in_=turned[:, 0 : VECTORS * BLOCKS]
-            )
-            nc.vector.tensor_scalar_add(out=dt_b_shifted[:], in0=params[:, V_DT_B, :], scalar1=DT_MIN)
-            nc.vector.tensor_scalar_mul(out=z_b_half[:], in0=params[:, V_Z_B, :], scalar1=0.5)
-            nc.vector.tensor_scalar_max(out=a_floor[:], in0=params[:, V_A_BASE, :], scalar1=SOFTPLUS_FLOOR)
+        vectors_turned = psum_scalar.tile([P, P], BF16, tag="scalar")
+        nc.tensor.transpose(vectors_turned[:], vector_rows[:], ident_bf16[:])
+        nc.vector.tensor_copy(
+            out=params[:].rearrange("p v j -> p (v j)"), in_=vectors_turned[:, 0 : VECTORS * BLOCKS]
+        )
+        nc.vector.tensor_scalar_add(out=dt_b_shifted[:], in0=params[:, V_DT_B, :], scalar1=DT_MIN)
+        nc.vector.tensor_scalar_mul(out=z_b_half[:], in0=params[:, V_Z_B, :], scalar1=0.5)
+        nc.vector.tensor_scalar_max(out=a_floor[:], in0=params[:, V_A_BASE, :], scalar1=SOFTPLUS_FLOOR)
+        nc.scalar.activation(out=a_log[:], in_=a_floor[:], func=FUNC.Exp, scale=-1.0)
 
         grouped_of = {}
         dt_of = {}
         log_of = {}
         b_of = {}
-        gate_of = {}
         decay_of = {}
-        o_of = {}
+        gate_of = {}
+        back_of = {}
         sumsq_of = {}
         rstd_of = {}
 
-        def live(c):
-            return 0 <= c < CHUNKS
+        def block_tile(tag, first_lag, last_lag):
+            fresh = work.tile([P, CHUNK], F32, tag=tag, bufs=slots(first_lag, last_lag))
+            return fresh
+
+        def column(tag):
+            fresh = work.tile([P, 1], F32, tag=tag, bufs=4)
+            return fresh
 
         def project(pool, tag, w, c, j):
             acc = pool.tile([P, CHUNK], F32, tag=tag)
@@ -173,185 +200,182 @@ def tile_mamba2backbone_pb_t_kernel(
             )
             return acc
 
-        def turn_x_for_quantising(c):
-            grouped = stage.tile([P, CHUNK, 4], BF16, tag="grouped", align_bytes=64)
-            grouped_of[c] = grouped
-            grouped_words = (
-                grouped[:]
-                .rearrange("p r t -> p (r t)")
-                .bitcast(F32)
-                .rearrange("p (n r u) -> p n r u", n=TILES_PER_CHUNK, r=P, u=2)
+        def turn_x(c, t):
+            grouped = work.tile(
+                [P, P, 4], BF16, tag="grouped", bufs=slots(LAG_TURN_X, LAG_QUANTISE), align_bytes=64
             )
-            for half in range(2):
-                turned = psum_scalar.tile([P, 2, 2, P], F32, tag="scalar")
-                for m in range(2):
-                    words = x_sb[:, c * TILES_PER_CHUNK + 2 * half + m, :].bitcast(F32)
-                    for u in range(2):
-                        nc.tensor.transpose(turned[:, m, u, :], words[:, u:WORDS:2], ident_f32[:])
-                nc.scalar.copy(
-                    out=grouped_words[:, 2 * half : 2 * half + 2, :, :],
-                    in_=turned[:].rearrange("p m u r -> p m r u"),
-                )
+            grouped_of[(c, t)] = grouped
+            words = x_sb[:, c * QUARTERS + t, :].bitcast(F32)
+            turned = psum_words.tile([P, 2, P], F32, tag="words")
+            for u in range(2):
+                nc.tensor.transpose(turned[:, u, :], words[:, u:WORDS:2], ident_f32[:])
+            nc.vector.tensor_copy(
+                out=grouped[:].rearrange("p r t -> p (r t)").bitcast(F32).rearrange("p (r u) -> p r u", u=2),
+                in_=turned[:].rearrange("p u r -> p r u"),
+            )
 
-        def quantise_x(c):
+        def quantise_x(c, t):
             nc.vector.quantize_mx(
-                out=x_codes[:, c, :].bitcast(FP8X4),
-                scales=x_planes[:, c, :],
-                in_=grouped_of[c][:].rearrange("p r t -> p (r t)"),
+                out=x_codes[:, c, block(t)].bitcast(FP8X4),
+                scales=x_planes[:, c, block(t)],
+                in_=grouped_of[(c, t)][:].rearrange("p r t -> p (r t)"),
             )
 
-        def floor_dt_input(c):
-            dt = work.tile([P, BLOCKS, CHUNK], F32, tag="dt")
-            dt_of[c] = dt
-            for j in range(BLOCKS):
-                acc = project(psum_vector, "vector", W_DT, c, j)
-                nc.vector.tensor_scalar(
-                    out=dt[:, j, :],
-                    in0=acc[:],
-                    scalar1=dt_b_shifted[:, j : j + 1],
-                    scalar2=SOFTPLUS_FLOOR,
-                    op0=ALU.add,
-                    op1=ALU.max,
-                )
-
-        def exp_and_tanh(c, j):
-            nc.scalar.activation(
-                out=log_of[c][:, j, :], in_=dt_of[c][:, j, :], func=FUNC.Exp, scale=-1.0, bias=dt_min_col[:]
-            )
-            acc_b = project(psum_scalar, "scalar", W_B, c, j)
-            nc.scalar.activation(
-                out=b_of[c][:, j, :], in_=acc_b[:], func=FUNC.Tanh, bias=params[:, V_B_B, j : j + 1]
-            )
-            acc_z = project(psum_scalar, "scalar", W_Z, c, j)
-            nc.scalar.activation(
-                out=gate_of[c][:, j, :], in_=acc_z[:], func=FUNC.Tanh, scale=0.5, bias=z_b_half[:, j : j + 1]
+        def floor_dt_input(c, j):
+            dt = block_tile("dt", LAG_FLOOR, LAG_DECAY)
+            dt_of[(c, j)] = dt
+            acc = project(psum_vector, "vector", W_DT, c, j)
+            nc.vector.tensor_scalar(
+                out=dt[:],
+                in0=acc[:],
+                scalar1=dt_b_shifted[:, j : j + 1],
+                scalar2=SOFTPLUS_FLOOR,
+                op0=ALU.add,
+                op1=ALU.max,
             )
 
-        def finish_dt(c):
-            dt, log, b = dt_of[c], log_of[c], b_of[c]
-            decay = work.tile([P, BLOCKS, CHUNK], F32, tag="decay")
-            decay_of[c] = decay
-            for j in range(BLOCKS):
-                nc.gpsimd.tensor_tensor(out=dt[:, j, :], in0=dt[:, j, :], in1=log[:, j, :], op=ALU.add)
-            for j in range(BLOCKS):
-                nc.scalar.activation(
-                    out=decay[:, j, :], in_=dt[:, j, :], func=FUNC.Exp, scale=a_neg[:, j : j + 1]
+        def exp_of_minus_m(c, j):
+            log = block_tile("log", LAG_EXP, LAG_DT)
+            log_of[(c, j)] = log
+            nc.scalar.activation(
+                out=log[:], in_=dt_of[(c, j)][:], func=FUNC.Exp, scale=-1.0, bias=dt_min_col[:]
+            )
+
+        def logs_of_chunk(c):
+            if c == 0:
+                nc.scalar.activation(out=a_log[:], in_=a_log[:], func=FUNC.Ln, bias=one_col[:])
+                nc.vector.scalar_tensor_tensor(
+                    out=a_neg[:], in0=a_floor[:], scalar=-1.0, in1=a_log[:], op0=ALU.mult, op1=ALU.subtract
                 )
             for j in range(BLOCKS):
-                nc.gpsimd.tensor_tensor(out=b[:, j, :], in0=dt[:, j, :], in1=b[:, j, :], op=ALU.mult)
+                log = log_of[(c, j)]
+                nc.scalar.activation(out=log[:], in_=log[:], func=FUNC.Ln, bias=one_col[:])
+
+        def tanh_b(c, j):
+            b = block_tile("b", LAG_TANH_B, LAG_SUM)
+            b_of[(c, j)] = b
+            acc = project(psum_scalar, "scalar", W_B, c, j)
+            nc.scalar.activation(out=b[:], in_=acc[:], func=FUNC.Tanh, bias=params[:, V_B_B, j : j + 1])
+
+        def finish_dt(c, j):
+            dt, b = dt_of[(c, j)], b_of[(c, j)]
+            nc.gpsimd.tensor_tensor(out=dt[:], in0=dt[:], in1=log_of[(c, j)][:], op=ALU.add)
+            nc.gpsimd.tensor_tensor(out=b[:], in0=dt[:], in1=b[:], op=ALU.mult)
+
+        def decay(c, j):
+            d_a = block_tile("decay", LAG_DECAY, LAG_GATE)
+            decay_of[(c, j)] = d_a
+            nc.scalar.activation(
+                out=d_a[:], in_=dt_of[(c, j)][:], func=FUNC.Exp, scale=a_neg[:, j : j + 1]
+            )
 
         def state_terms(c, j):
-            deter_term, x_term = decay_of[c][:, j, :], b_of[c][:, j, :]
-            acc_c = project(psum_vector, "vector", W_C, c, j)
+            deter_term, x_term = decay_of[(c, j)], b_of[(c, j)]
+            acc = project(psum_vector, "vector", W_C, c, j)
             turned = psum_turned.tile([P, 2, CHUNK], BF16, tag="turned")
             for side, source in enumerate((x_sb, deter_sb)):
-                for t in range(TILES_PER_CHUNK):
+                for t in range(QUARTERS):
                     nc.tensor.transpose(
-                        turned[:, side, block(t)],
-                        source[:, c * TILES_PER_CHUNK + t, block(j)],
-                        ident_bf16[:],
+                        turned[:, side, block(t)], source[:, c * QUARTERS + t, block(j)], ident_bf16[:]
                     )
             c_bias = params[:, V_C_B, j : j + 1]
             nc.vector.scalar_tensor_tensor(
-                out=deter_term, in0=acc_c[:], scalar=c_bias, in1=deter_term, op0=ALU.add, op1=ALU.mult
+                out=deter_term[:], in0=acc[:], scalar=c_bias, in1=deter_term[:], op0=ALU.add, op1=ALU.mult
             )
             nc.vector.scalar_tensor_tensor(
-                out=deter_term, in0=deter_term, scalar=-1.0, in1=turned[:, 1, :], op0=ALU.add, op1=ALU.mult
+                out=x_term[:], in0=acc[:], scalar=c_bias, in1=x_term[:], op0=ALU.add, op1=ALU.mult
             )
             nc.vector.scalar_tensor_tensor(
-                out=x_term, in0=acc_c[:], scalar=c_bias, in1=x_term, op0=ALU.add, op1=ALU.mult
+                out=deter_term[:], in0=deter_term[:], scalar=-1.0, in1=turned[:, 1, :], op0=ALU.add, op1=ALU.mult
             )
             nc.vector.scalar_tensor_tensor(
-                out=x_term,
-                in0=x_term,
+                out=x_term[:],
+                in0=x_term[:],
                 scalar=params[:, V_SKIP, j : j + 1],
                 in1=turned[:, 0, :],
                 op0=ALU.add,
                 op1=ALU.mult,
             )
-            nc.gpsimd.tensor_tensor(out=deter_term, in0=deter_term, in1=x_term, op=ALU.add)
+
+        def sum_terms(c, j):
+            s = decay_of[(c, j)]
+            nc.gpsimd.tensor_tensor(out=s[:], in0=s[:], in1=b_of[(c, j)][:], op=ALU.add)
+
+        def tanh_z(c, j):
+            gate = block_tile("gate", LAG_TANH_Z, LAG_BACK + QUARTERS - 1)
+            gate_of[(c, j)] = gate
+            acc = project(psum_scalar, "scalar", W_Z, c, j)
+            nc.scalar.activation(
+                out=gate[:], in_=acc[:], func=FUNC.Tanh, scale=0.5, bias=z_b_half[:, j : j + 1]
+            )
 
         def apply_gate(c, j):
-            gate = gate_of[c][:, j, :]
+            gate = gate_of[(c, j)]
             nc.vector.scalar_tensor_tensor(
-                out=gate, in0=gate, scalar=1.0, in1=decay_of[c][:, j, :], op0=ALU.add, op1=ALU.mult
+                out=gate[:], in0=gate[:], scalar=1.0, in1=decay_of[(c, j)][:], op0=ALU.add, op1=ALU.mult
             )
 
-        def back_to_token_rows(c):
-            o = rows.tile([P, TILES_PER_CHUNK, CHANNELS], F32, tag="o")
-            sumsq = rows.tile([P, TILES_PER_CHUNK], F32, tag="sumsq")
-            o_of[c], sumsq_of[c] = o, sumsq
-            for t in range(TILES_PER_CHUNK):
-                back = psum_back.tile([P, CHANNELS], F32, tag="back")
-                for j in range(BLOCKS):
-                    nc.tensor.transpose(back[:, block(j)], gate_of[c][:, j, block(t)], ident_f32[:])
-                nc.vector.scalar_tensor_tensor(
-                    out=o[:, t, :],
-                    in0=back[:],
-                    scalar=0.5,
-                    in1=deter_sb[:, c * TILES_PER_CHUNK + t, :],
-                    op0=ALU.mult,
-                    op1=ALU.add,
+        def back_to_rows(c, t):
+            back = psum_back.tile([P, CHANNELS], F32, tag="back")
+            back_of[(c, t)] = back
+            nc.tensor.matmul(
+                out=back[:], lhsT=twice_ident[:], rhs=deter_sb[:, c * QUARTERS + t, :], start=True, stop=False
+            )
+            for j in range(BLOCKS):
+                nc.tensor.matmul(
+                    out=back[:, block(j)],
+                    lhsT=gate_of[(c, j)][:, block(t)],
+                    rhs=ident_f32[:],
+                    is_transpose=True,
+                    start=False,
+                    stop=(j == BLOCKS - 1),
                 )
-                squares = stage.tile([P, CHANNELS], BF16, tag="squares")
-                nc.scalar.activation(
-                    out=squares[:], in_=o[:, t, :], func=FUNC.Square, accum_out=sumsq[:, t : t + 1]
-                )
+            sumsq = column("sumsq")
+            sumsq_of[(c, t)] = sumsq
+            squares = work.tile([P, CHANNELS], BF16, tag="squares")
+            nc.scalar.activation(
+                out=squares[:], in_=back[:], func=FUNC.Square, scale=CHANNELS**-0.5, accum_out=sumsq[:]
+            )
+
+        def one_over_root(c, t):
+            shifted = column("shifted")
+            rstd = column("rstd")
+            rstd_of[(c, t)] = rstd
+            nc.vector.tensor_scalar_add(out=shifted[:], in0=sumsq_of[(c, t)][:], scalar1=4.0 * EPS)
+            nc.gpsimd.tensor_tensor(out=rstd[:], in0=shifted[:], in1=minus_half_col[:], op=ALU.pow)
 
         def normalise(c, t):
-            o = o_of[c][:, t, :]
+            result = work.tile([P, CHANNELS], F32, tag="result", bufs=4)
             nc.vector.scalar_tensor_tensor(
-                out=o, in0=o, scalar=rstd_of[c][:, t : t + 1], in1=norm_w_all[:], op0=ALU.mult, op1=ALU.mult
+                out=result[:],
+                in0=back_of[(c, t)][:],
+                scalar=rstd_of[(c, t)][:],
+                in1=norm_w_all[:],
+                op0=ALU.mult,
+                op1=ALU.mult,
             )
+            nc.sync.dma_start(out=out_rows[:, c * QUARTERS + t, :], in_=result[:])
 
-        FIRST_PASS = -2
-        for i in range(FIRST_PASS, CHUNKS + 2):
-            if i == FIRST_PASS + 1:
-                prepare_parameters()
-            if live(i - 2):
-                rstd = rows.tile([P, TILES_PER_CHUNK], F32, tag="rstd")
-                rstd_of[i - 2] = rstd
-                nc.scalar.activation(out=rstd[:], in_=sumsq_of[i - 2][:], func=FUNC.Exp, scale=-0.5)
-            if live(i):
-                finish_dt(i)
-            if live(i + 1):
-                quantise_x(i + 1)
-            if live(i - 1):
-                back_to_token_rows(i - 1)
-            if live(i + 1):
-                floor_dt_input(i + 1)
-                log_next = work.tile([P, BLOCKS, CHUNK], F32, tag="log")
-                b_next = work.tile([P, BLOCKS, CHUNK], F32, tag="b")
-                gate_next = work.tile([P, BLOCKS, CHUNK], F32, tag="gate")
-                log_of[i + 1], b_of[i + 1], gate_of[i + 1] = log_next, b_next, gate_next
-            if live(i + 2):
-                turn_x_for_quantising(i + 2)
-            for j in range(BLOCKS):
-                if live(i):
-                    state_terms(i, j)
-                    if j > 0:
-                        apply_gate(i, j - 1)
-                if live(i + 1):
-                    exp_and_tanh(i + 1, j)
-            for t in range(TILES_PER_CHUNK):
-                if t == TILES_PER_CHUNK // 2 and live(i):
-                    apply_gate(i, BLOCKS - 1)
-                if live(i - 2):
-                    normalise(i - 2, t)
-            if live(i - 2):
-                nc.sync.dma_start(out=out_rows[:, chunk_tiles(i - 2), :], in_=o_of[i - 2][:])
-            if i == FIRST_PASS + 1:
-                nc.scalar.activation(out=a_exp[:], in_=a_floor[:], func=FUNC.Exp, scale=-1.0)
-                nc.scalar.activation(out=a_exp[:], in_=a_exp[:], func=FUNC.Ln, bias=one_col[:])
-                nc.vector.scalar_tensor_tensor(
-                    out=a_neg[:], in0=a_floor[:], scalar=-1.0, in1=a_exp[:], op0=ALU.mult, op1=ALU.subtract
-                )
-            if live(i + 1):
-                for j in range(BLOCKS):
-                    log = log_of[i + 1][:, j, :]
-                    nc.scalar.activation(out=log, in_=log, func=FUNC.Ln, bias=one_col[:])
-            if live(i - 1):
-                sumsq = sumsq_of[i - 1]
-                nc.scalar.activation(
-                    out=sumsq[:], in_=sumsq[:], func=FUNC.Ln, scale=1.0 / CHANNELS, bias=eps_col[:]
-                )
+        def at(step, lag, stage):
+            unit = step - lag
+            if 0 <= unit < UNITS:
+                stage(unit // QUARTERS, unit % QUARTERS)
+
+        for step in range(LAG_TURN_X, UNITS + LAG_NORM):
+            at(step, LAG_SUM, sum_terms)
+            at(step, LAG_DT, finish_dt)
+            at(step, LAG_DECAY, decay)
+            at(step, LAG_TERMS, state_terms)
+            at(step, LAG_NORM, one_over_root)
+            at(step, LAG_TANH_Z, tanh_z)
+            at(step, LAG_GATE, apply_gate)
+            at(step, LAG_QUANTISE, quantise_x)
+            at(step, LAG_TANH_B, tanh_b)
+            at(step, LAG_FLOOR, floor_dt_input)
+            at(step, LAG_EXP, exp_of_minus_m)
+            at(step, LAG_BACK, back_to_rows)
+            at(step, LAG_TURN_X, turn_x)
+            at(step, LAG_NORM, normalise)
+            last_exp = step - LAG_EXP
+            if 0 <= last_exp < UNITS and last_exp % BLOCKS == BLOCKS - 1:
+                logs_of_chunk(last_exp // BLOCKS)

@@ -32,8 +32,8 @@ W_DT, W_B, W_C, W_Z = 0, 1, 2, 3
 V_DT_B, V_B_B, V_C_B, V_Z_B, V_A_BASE, V_SKIP = 0, 1, 2, 3, 4, 5
 VECTORS = 6
 
-LAG_TURN_X = -6
-LAG_QUANTISE = -5
+LAG_TURN_X = -5
+LAG_QUANTISE = -4
 LAG_FLOOR = -1
 LAG_EXP = 0
 LAG_TANH_B = 3
@@ -45,7 +45,7 @@ LAG_TANH_Z = 7
 LAG_GATE = 8
 LAG_BACK = 12
 LAG_NORM = 13
-assert LAG_FLOOR - LAG_QUANTISE >= QUARTERS
+assert LAG_FLOOR - LAG_QUANTISE >= QUARTERS - 1
 assert LAG_DT - LAG_EXP >= BLOCKS
 assert LAG_BACK - LAG_GATE >= BLOCKS
 
@@ -148,9 +148,11 @@ def tile_mamba2backbone_pb_t_kernel(
         one_col = keep.tile([P, 1], F32)
         dt_min_col = keep.tile([P, 1], F32)
         minus_half_col = keep.tile([P, 1], F32)
+        four_eps_col = keep.tile([P, 1], F32)
         nc.vector.memset(one_col[:], 1.0)
         nc.vector.memset(dt_min_col[:], DT_MIN)
         nc.vector.memset(minus_half_col[:], -0.5)
+        nc.vector.memset(four_eps_col[:], 4.0 * EPS)
 
         params = keep.tile([P, VECTORS, BLOCKS], F32)
         dt_b_shifted = keep.tile([P, BLOCKS], F32)
@@ -159,15 +161,16 @@ def tile_mamba2backbone_pb_t_kernel(
         a_log = keep.tile([P, BLOCKS], F32)
         a_neg = keep.tile([P, BLOCKS], F32)
 
-        vectors_turned = psum_scalar.tile([P, P], BF16, tag="scalar")
-        nc.tensor.transpose(vectors_turned[:], vector_rows[:], ident_bf16[:])
-        nc.vector.tensor_copy(
-            out=params[:].rearrange("p v j -> p (v j)"), in_=vectors_turned[:, 0 : VECTORS * BLOCKS]
-        )
-        nc.vector.tensor_scalar_add(out=dt_b_shifted[:], in0=params[:, V_DT_B, :], scalar1=DT_MIN)
-        nc.vector.tensor_scalar_mul(out=z_b_half[:], in0=params[:, V_Z_B, :], scalar1=0.5)
-        nc.vector.tensor_scalar_max(out=a_floor[:], in0=params[:, V_A_BASE, :], scalar1=SOFTPLUS_FLOOR)
-        nc.scalar.activation(out=a_log[:], in_=a_floor[:], func=FUNC.Exp, scale=-1.0)
+        def prepare_parameters():
+            vectors_turned = psum_scalar.tile([P, P], BF16, tag="scalar")
+            nc.tensor.transpose(vectors_turned[:], vector_rows[:], ident_bf16[:])
+            nc.vector.tensor_copy(
+                out=params[:].rearrange("p v j -> p (v j)"), in_=vectors_turned[:, 0 : VECTORS * BLOCKS]
+            )
+            nc.vector.tensor_scalar_add(out=dt_b_shifted[:], in0=params[:, V_DT_B, :], scalar1=DT_MIN)
+            nc.vector.tensor_scalar_mul(out=z_b_half[:], in0=params[:, V_Z_B, :], scalar1=0.5)
+            nc.vector.tensor_scalar_max(out=a_floor[:], in0=params[:, V_A_BASE, :], scalar1=SOFTPLUS_FLOOR)
+            nc.scalar.activation(out=a_log[:], in_=a_floor[:], func=FUNC.Exp, scale=-1.0)
 
         grouped_of = {}
         dt_of = {}
@@ -176,7 +179,7 @@ def tile_mamba2backbone_pb_t_kernel(
         decay_of = {}
         gate_of = {}
         back_of = {}
-        sumsq_of = {}
+        mean_of = {}
         rstd_of = {}
 
         def block_tile(tag, first_lag, last_lag):
@@ -201,24 +204,24 @@ def tile_mamba2backbone_pb_t_kernel(
             return acc
 
         def turn_x(c, t):
-            grouped = work.tile(
-                [P, P, 4], BF16, tag="grouped", bufs=slots(LAG_TURN_X, LAG_QUANTISE), align_bytes=64
-            )
-            grouped_of[(c, t)] = grouped
+            if t == 0:
+                fresh = work.tile([P, CHUNK, 4], BF16, tag="grouped", align_bytes=64)
+                grouped_of[c] = fresh
+            grouped = grouped_of[c][:, block(t), :]
             words = x_sb[:, c * QUARTERS + t, :].bitcast(F32)
             turned = psum_words.tile([P, 2, P], F32, tag="words")
             for u in range(2):
                 nc.tensor.transpose(turned[:, u, :], words[:, u:WORDS:2], ident_f32[:])
             nc.vector.tensor_copy(
-                out=grouped[:].rearrange("p r t -> p (r t)").bitcast(F32).rearrange("p (r u) -> p r u", u=2),
+                out=grouped.rearrange("p r t -> p (r t)").bitcast(F32).rearrange("p (r u) -> p r u", u=2),
                 in_=turned[:].rearrange("p u r -> p r u"),
             )
 
-        def quantise_x(c, t):
+        def quantise_chunk(c):
             nc.vector.quantize_mx(
-                out=x_codes[:, c, block(t)].bitcast(FP8X4),
-                scales=x_planes[:, c, block(t)],
-                in_=grouped_of[(c, t)][:].rearrange("p r t -> p (r t)"),
+                out=x_codes[:, c, :].bitcast(FP8X4),
+                scales=x_planes[:, c, :],
+                in_=grouped_of[c][:].rearrange("p r t -> p (r t)"),
             )
 
         def floor_dt_input(c, j):
@@ -263,7 +266,7 @@ def tile_mamba2backbone_pb_t_kernel(
             nc.gpsimd.tensor_tensor(out=b[:], in0=dt[:], in1=b[:], op=ALU.mult)
 
         def decay(c, j):
-            d_a = block_tile("decay", LAG_DECAY, LAG_GATE)
+            d_a = block_tile("decay", LAG_DECAY, LAG_GATE + BLOCKS - 1)
             decay_of[(c, j)] = d_a
             nc.scalar.activation(
                 out=d_a[:], in_=dt_of[(c, j)][:], func=FUNC.Exp, scale=a_neg[:, j : j + 1]
@@ -309,11 +312,12 @@ def tile_mamba2backbone_pb_t_kernel(
                 out=gate[:], in_=acc[:], func=FUNC.Tanh, scale=0.5, bias=z_b_half[:, j : j + 1]
             )
 
-        def apply_gate(c, j):
-            gate = gate_of[(c, j)]
-            nc.vector.scalar_tensor_tensor(
-                out=gate[:], in0=gate[:], scalar=1.0, in1=decay_of[(c, j)][:], op0=ALU.add, op1=ALU.mult
-            )
+        def gate_chunk(c):
+            for j in range(BLOCKS):
+                gate = gate_of[(c, j)]
+                nc.vector.scalar_tensor_tensor(
+                    out=gate[:], in0=gate[:], scalar=1.0, in1=decay_of[(c, j)][:], op0=ALU.add, op1=ALU.mult
+                )
 
         def back_to_rows(c, t):
             back = psum_back.tile([P, CHANNELS], F32, tag="back")
@@ -330,19 +334,18 @@ def tile_mamba2backbone_pb_t_kernel(
                     start=False,
                     stop=(j == BLOCKS - 1),
                 )
-            sumsq = column("sumsq")
-            sumsq_of[(c, t)] = sumsq
+            mean = column("mean")
+            mean_of[(c, t)] = mean
             squares = work.tile([P, CHANNELS], BF16, tag="squares")
             nc.scalar.activation(
-                out=squares[:], in_=back[:], func=FUNC.Square, scale=CHANNELS**-0.5, accum_out=sumsq[:]
+                out=squares[:], in_=back[:], func=FUNC.Square, scale=CHANNELS**-0.5, accum_out=mean[:]
             )
+            nc.scalar.activation(out=mean[:], in_=mean[:], func=FUNC.Identity, bias=four_eps_col[:])
 
         def one_over_root(c, t):
-            shifted = column("shifted")
             rstd = column("rstd")
             rstd_of[(c, t)] = rstd
-            nc.vector.tensor_scalar_add(out=shifted[:], in0=sumsq_of[(c, t)][:], scalar1=4.0 * EPS)
-            nc.gpsimd.tensor_tensor(out=rstd[:], in0=shifted[:], in1=minus_half_col[:], op=ALU.pow)
+            nc.gpsimd.tensor_tensor(out=rstd[:], in0=mean_of[(c, t)][:], in1=minus_half_col[:], op=ALU.pow)
 
         def normalise(c, t):
             result = work.tile([P, CHANNELS], F32, tag="result", bufs=4)
@@ -361,21 +364,30 @@ def tile_mamba2backbone_pb_t_kernel(
             if 0 <= unit < UNITS:
                 stage(unit // QUARTERS, unit % QUARTERS)
 
-        for step in range(LAG_TURN_X, UNITS + LAG_NORM):
+        def at_end_of_chunk(step, lag, stage):
+            unit = step - lag
+            if 0 <= unit < UNITS and unit % QUARTERS == QUARTERS - 1:
+                stage(unit // QUARTERS)
+
+        def run_step(step):
+            at(step, LAG_NORM, one_over_root)
             at(step, LAG_SUM, sum_terms)
             at(step, LAG_DT, finish_dt)
             at(step, LAG_DECAY, decay)
             at(step, LAG_TERMS, state_terms)
-            at(step, LAG_NORM, one_over_root)
             at(step, LAG_TANH_Z, tanh_z)
-            at(step, LAG_GATE, apply_gate)
-            at(step, LAG_QUANTISE, quantise_x)
+            at_end_of_chunk(step, LAG_GATE, gate_chunk)
+            at_end_of_chunk(step, LAG_QUANTISE, quantise_chunk)
             at(step, LAG_TANH_B, tanh_b)
-            at(step, LAG_FLOOR, floor_dt_input)
-            at(step, LAG_EXP, exp_of_minus_m)
             at(step, LAG_BACK, back_to_rows)
             at(step, LAG_TURN_X, turn_x)
             at(step, LAG_NORM, normalise)
-            last_exp = step - LAG_EXP
-            if 0 <= last_exp < UNITS and last_exp % BLOCKS == BLOCKS - 1:
-                logs_of_chunk(last_exp // BLOCKS)
+            at(step, LAG_FLOOR, floor_dt_input)
+            at(step, LAG_EXP, exp_of_minus_m)
+            at_end_of_chunk(step, LAG_EXP, logs_of_chunk)
+
+        for step in range(LAG_TURN_X, LAG_FLOOR):
+            run_step(step)
+        prepare_parameters()
+        for step in range(LAG_FLOOR, UNITS + LAG_NORM):
+            run_step(step)

@@ -36,8 +36,8 @@ LAG_TURN_X = -5
 LAG_QUANTISE = -4
 LAG_FLOOR = -1
 LAG_EXP = 0
-LAG_TANH_B = 3
-LAG_DT = 4
+LAG_TANH_B = 2
+LAG_DT = 3
 LAG_DECAY = 5
 LAG_TERMS = 6
 LAG_SUM = 7
@@ -46,14 +46,14 @@ LAG_GATE = 8
 LAG_BACK = 12
 LAG_NORM = 13
 assert LAG_FLOOR - LAG_QUANTISE >= QUARTERS - 1
-assert LAG_DT - LAG_EXP >= BLOCKS
+assert LAG_DT + 1 - LAG_EXP >= BLOCKS
 assert LAG_BACK - LAG_GATE >= BLOCKS
 
 FLOPS = 2 * TOKENS * CHANNELS * CHANNELS * 4
 
 
-def slots(first_lag, last_lag):
-    return last_lag - first_lag + 2
+def pair_slots(first_lag, last_lag):
+    return (last_lag - first_lag + 1) // 2 + 2
 
 
 def tile_mamba2backbone_pb_t_kernel(
@@ -82,11 +82,9 @@ def tile_mamba2backbone_pb_t_kernel(
         ctx.enter_context(tc.manual_schedule())
         keep = ctx.enter_context(tc.tile_pool(name="keep", bufs=1))
         work = ctx.enter_context(tc.tile_pool(name="work", bufs=2))
-        psum_scalar = ctx.enter_context(tc.psum_pool(name="psum_scalar", bufs=2))
+        psum_scalar = ctx.enter_context(tc.psum_pool(name="psum_scalar", bufs=4))
         psum_vector = ctx.enter_context(tc.psum_pool(name="psum_vector", bufs=2))
-        psum_words = ctx.enter_context(tc.psum_pool(name="psum_words", bufs=1))
-        psum_turned = ctx.enter_context(tc.psum_pool(name="psum_turned", bufs=1))
-        psum_back = ctx.enter_context(tc.psum_pool(name="psum_back", bufs=2))
+        psum_turned = ctx.enter_context(tc.psum_pool(name="psum_turned", bufs=2))
 
         x_rows = x.rearrange("(p n) c -> p n c", n=TILES)
         deter_rows = deter.rearrange("(p n) c -> p n c", n=TILES)
@@ -182,9 +180,17 @@ def tile_mamba2backbone_pb_t_kernel(
         mean_of = {}
         rstd_of = {}
 
-        def block_tile(tag, first_lag, last_lag):
-            fresh = work.tile([P, CHUNK], F32, tag=tag, bufs=slots(first_lag, last_lag))
-            return fresh
+        def block_of(tiles, tag, first_lag, last_lag, c, j):
+            if j % 2 == 0:
+                fresh = work.tile([P, 2, CHUNK], F32, tag=tag, bufs=pair_slots(first_lag, last_lag))
+                tiles[(c, j // 2)] = fresh
+            return tiles[(c, j // 2)][:, j % 2, :]
+
+        def old_block(tiles, c, j):
+            return tiles[(c, j // 2)][:, j % 2, :]
+
+        def whole_pair(tiles, c, pair):
+            return tiles[(c, pair)][:].rearrange("p h n -> p (h n)")
 
         def column(tag):
             fresh = work.tile([P, 1], F32, tag=tag, bufs=4)
@@ -209,7 +215,7 @@ def tile_mamba2backbone_pb_t_kernel(
                 grouped_of[c] = fresh
             grouped = grouped_of[c][:, block(t), :]
             words = x_sb[:, c * QUARTERS + t, :].bitcast(F32)
-            turned = psum_words.tile([P, 2, P], F32, tag="words")
+            turned = psum_turned.tile([P, 2, P], F32, tag="turned")
             for u in range(2):
                 nc.tensor.transpose(turned[:, u, :], words[:, u:WORDS:2], ident_f32[:])
             nc.vector.tensor_copy(
@@ -225,11 +231,10 @@ def tile_mamba2backbone_pb_t_kernel(
             )
 
         def floor_dt_input(c, j):
-            dt = block_tile("dt", LAG_FLOOR, LAG_DECAY)
-            dt_of[(c, j)] = dt
+            dt = block_of(dt_of, "dt", LAG_FLOOR, LAG_DECAY, c, j)
             acc = project(psum_vector, "vector", W_DT, c, j)
             nc.vector.tensor_scalar(
-                out=dt[:],
+                out=dt,
                 in0=acc[:],
                 scalar1=dt_b_shifted[:, j : j + 1],
                 scalar2=SOFTPLUS_FLOOR,
@@ -238,10 +243,9 @@ def tile_mamba2backbone_pb_t_kernel(
             )
 
         def exp_of_minus_m(c, j):
-            log = block_tile("log", LAG_EXP, LAG_DT)
-            log_of[(c, j)] = log
+            log = block_of(log_of, "log", LAG_EXP, LAG_DT, c, j)
             nc.scalar.activation(
-                out=log[:], in_=dt_of[(c, j)][:], func=FUNC.Exp, scale=-1.0, bias=dt_min_col[:]
+                out=log, in_=old_block(dt_of, c, j), func=FUNC.Exp, scale=-1.0, bias=dt_min_col[:]
             )
 
         def logs_of_chunk(c):
@@ -250,30 +254,28 @@ def tile_mamba2backbone_pb_t_kernel(
                 nc.vector.scalar_tensor_tensor(
                     out=a_neg[:], in0=a_floor[:], scalar=-1.0, in1=a_log[:], op0=ALU.mult, op1=ALU.subtract
                 )
-            for j in range(BLOCKS):
-                log = log_of[(c, j)]
-                nc.scalar.activation(out=log[:], in_=log[:], func=FUNC.Ln, bias=one_col[:])
+            for pair in range(BLOCKS // 2):
+                log = whole_pair(log_of, c, pair)
+                nc.scalar.activation(out=log, in_=log, func=FUNC.Ln, bias=one_col[:])
 
         def tanh_b(c, j):
-            b = block_tile("b", LAG_TANH_B, LAG_SUM)
-            b_of[(c, j)] = b
+            b = block_of(b_of, "b", LAG_TANH_B, LAG_SUM, c, j)
             acc = project(psum_scalar, "scalar", W_B, c, j)
-            nc.scalar.activation(out=b[:], in_=acc[:], func=FUNC.Tanh, bias=params[:, V_B_B, j : j + 1])
+            nc.scalar.activation(out=b, in_=acc[:], func=FUNC.Tanh, bias=params[:, V_B_B, j : j + 1])
 
-        def finish_dt(c, j):
-            dt, b = dt_of[(c, j)], b_of[(c, j)]
-            nc.gpsimd.tensor_tensor(out=dt[:], in0=dt[:], in1=log_of[(c, j)][:], op=ALU.add)
-            nc.gpsimd.tensor_tensor(out=b[:], in0=dt[:], in1=b[:], op=ALU.mult)
+        def finish_dt(c, pair):
+            dt, b = whole_pair(dt_of, c, pair), whole_pair(b_of, c, pair)
+            nc.gpsimd.tensor_tensor(out=dt, in0=dt, in1=whole_pair(log_of, c, pair), op=ALU.add)
+            nc.gpsimd.tensor_tensor(out=b, in0=dt, in1=b, op=ALU.mult)
 
         def decay(c, j):
-            d_a = block_tile("decay", LAG_DECAY, LAG_GATE + BLOCKS - 1)
-            decay_of[(c, j)] = d_a
+            d_a = block_of(decay_of, "decay", LAG_DECAY, LAG_GATE + BLOCKS - 1, c, j)
             nc.scalar.activation(
-                out=d_a[:], in_=dt_of[(c, j)][:], func=FUNC.Exp, scale=a_neg[:, j : j + 1]
+                out=d_a, in_=old_block(dt_of, c, j), func=FUNC.Exp, scale=a_neg[:, j : j + 1]
             )
 
         def state_terms(c, j):
-            deter_term, x_term = decay_of[(c, j)], b_of[(c, j)]
+            deter_term, x_term = old_block(decay_of, c, j), old_block(b_of, c, j)
             acc = project(psum_vector, "vector", W_C, c, j)
             turned = psum_turned.tile([P, 2, CHUNK], BF16, tag="turned")
             for side, source in enumerate((x_sb, deter_sb)):
@@ -283,44 +285,43 @@ def tile_mamba2backbone_pb_t_kernel(
                     )
             c_bias = params[:, V_C_B, j : j + 1]
             nc.vector.scalar_tensor_tensor(
-                out=deter_term[:], in0=acc[:], scalar=c_bias, in1=deter_term[:], op0=ALU.add, op1=ALU.mult
+                out=deter_term, in0=acc[:], scalar=c_bias, in1=deter_term, op0=ALU.add, op1=ALU.mult
             )
             nc.vector.scalar_tensor_tensor(
-                out=x_term[:], in0=acc[:], scalar=c_bias, in1=x_term[:], op0=ALU.add, op1=ALU.mult
+                out=x_term, in0=acc[:], scalar=c_bias, in1=x_term, op0=ALU.add, op1=ALU.mult
             )
             nc.vector.scalar_tensor_tensor(
-                out=deter_term[:], in0=deter_term[:], scalar=-1.0, in1=turned[:, 1, :], op0=ALU.add, op1=ALU.mult
+                out=deter_term, in0=deter_term, scalar=-1.0, in1=turned[:, 1, :], op0=ALU.add, op1=ALU.mult
             )
             nc.vector.scalar_tensor_tensor(
-                out=x_term[:],
-                in0=x_term[:],
+                out=x_term,
+                in0=x_term,
                 scalar=params[:, V_SKIP, j : j + 1],
                 in1=turned[:, 0, :],
                 op0=ALU.add,
                 op1=ALU.mult,
             )
 
-        def sum_terms(c, j):
-            s = decay_of[(c, j)]
-            nc.gpsimd.tensor_tensor(out=s[:], in0=s[:], in1=b_of[(c, j)][:], op=ALU.add)
+        def sum_terms(c, pair):
+            s = whole_pair(decay_of, c, pair)
+            nc.gpsimd.tensor_tensor(out=s, in0=s, in1=whole_pair(b_of, c, pair), op=ALU.add)
 
         def tanh_z(c, j):
-            gate = block_tile("gate", LAG_TANH_Z, LAG_BACK + QUARTERS - 1)
-            gate_of[(c, j)] = gate
+            gate = block_of(gate_of, "gate", LAG_TANH_Z, LAG_BACK + QUARTERS - 1, c, j)
             acc = project(psum_scalar, "scalar", W_Z, c, j)
             nc.scalar.activation(
-                out=gate[:], in_=acc[:], func=FUNC.Tanh, scale=0.5, bias=z_b_half[:, j : j + 1]
+                out=gate, in_=acc[:], func=FUNC.Tanh, scale=0.5, bias=z_b_half[:, j : j + 1]
             )
 
         def gate_chunk(c):
-            for j in range(BLOCKS):
-                gate = gate_of[(c, j)]
+            for pair in range(BLOCKS // 2):
+                gate = whole_pair(gate_of, c, pair)
                 nc.vector.scalar_tensor_tensor(
-                    out=gate[:], in0=gate[:], scalar=1.0, in1=decay_of[(c, j)][:], op0=ALU.add, op1=ALU.mult
+                    out=gate, in0=gate, scalar=1.0, in1=whole_pair(decay_of, c, pair), op0=ALU.add, op1=ALU.mult
                 )
 
         def back_to_rows(c, t):
-            back = psum_back.tile([P, CHANNELS], F32, tag="back")
+            back = psum_scalar.tile([P, CHANNELS], F32, tag="scalar")
             back_of[(c, t)] = back
             nc.tensor.matmul(
                 out=back[:], lhsT=twice_ident[:], rhs=deter_sb[:, c * QUARTERS + t, :], start=True, stop=False
@@ -328,7 +329,7 @@ def tile_mamba2backbone_pb_t_kernel(
             for j in range(BLOCKS):
                 nc.tensor.matmul(
                     out=back[:, block(j)],
-                    lhsT=gate_of[(c, j)][:, block(t)],
+                    lhsT=old_block(gate_of, c, j)[:, block(t)],
                     rhs=ident_f32[:],
                     is_transpose=True,
                     start=False,
@@ -364,6 +365,11 @@ def tile_mamba2backbone_pb_t_kernel(
             if 0 <= unit < UNITS:
                 stage(unit // QUARTERS, unit % QUARTERS)
 
+        def at_end_of_pair(step, lag, stage):
+            unit = step - lag
+            if 0 <= unit < UNITS and unit % 2 == 1:
+                stage(unit // QUARTERS, unit % QUARTERS // 2)
+
         def at_end_of_chunk(step, lag, stage):
             unit = step - lag
             if 0 <= unit < UNITS and unit % QUARTERS == QUARTERS - 1:
@@ -371,8 +377,8 @@ def tile_mamba2backbone_pb_t_kernel(
 
         def run_step(step):
             at(step, LAG_NORM, one_over_root)
-            at(step, LAG_SUM, sum_terms)
-            at(step, LAG_DT, finish_dt)
+            at_end_of_pair(step, LAG_DT, finish_dt)
+            at_end_of_pair(step, LAG_SUM, sum_terms)
             at(step, LAG_DECAY, decay)
             at(step, LAG_TERMS, state_terms)
             at(step, LAG_TANH_Z, tanh_z)

@@ -79,12 +79,21 @@ def tile_mamba2backbone_pb_t_kernel(
 ):
     nc = tc.nc
     with ExitStack() as ctx:
-        ctx.enter_context(tc.manual_schedule())
+        ctx.enter_context(
+            tc.manual_schedule(
+                engines={
+                    mybir.EngineType.Activation,
+                    mybir.EngineType.DVE,
+                    mybir.EngineType.Pool,
+                    mybir.EngineType.SP,
+                }
+            )
+        )
         keep = ctx.enter_context(tc.tile_pool(name="keep", bufs=1))
         work = ctx.enter_context(tc.tile_pool(name="work", bufs=2))
-        psum_scalar = ctx.enter_context(tc.psum_pool(name="psum_scalar", bufs=4))
-        psum_vector = ctx.enter_context(tc.psum_pool(name="psum_vector", bufs=2))
-        psum_turned = ctx.enter_context(tc.psum_pool(name="psum_turned", bufs=2))
+        psum_scalar = ctx.enter_context(tc.psum_pool(name="psum", bufs=8))
+        psum_vector = psum_scalar
+        psum_turned = psum_scalar
 
         x_rows = x.rearrange("(p n) c -> p n c", n=TILES)
         deter_rows = deter.rearrange("(p n) c -> p n c", n=TILES)
@@ -160,7 +169,7 @@ def tile_mamba2backbone_pb_t_kernel(
         a_neg = keep.tile([P, BLOCKS], F32)
 
         def prepare_parameters():
-            vectors_turned = psum_scalar.tile([P, P], BF16, tag="scalar")
+            vectors_turned = psum_scalar.tile([P, P], BF16, tag="bank")
             nc.tensor.transpose(vectors_turned[:], vector_rows[:], ident_bf16[:])
             nc.vector.tensor_copy(
                 out=params[:].rearrange("p v j -> p (v j)"), in_=vectors_turned[:, 0 : VECTORS * BLOCKS]
@@ -215,7 +224,7 @@ def tile_mamba2backbone_pb_t_kernel(
                 grouped_of[c] = fresh
             grouped = grouped_of[c][:, block(t), :]
             words = x_sb[:, c * QUARTERS + t, :].bitcast(F32)
-            turned = psum_turned.tile([P, 2, P], F32, tag="turned")
+            turned = psum_turned.tile([P, 2, P], F32, tag="bank")
             for u in range(2):
                 nc.tensor.transpose(turned[:, u, :], words[:, u:WORDS:2], ident_f32[:])
             nc.vector.tensor_copy(
@@ -232,7 +241,7 @@ def tile_mamba2backbone_pb_t_kernel(
 
         def floor_dt_input(c, j):
             dt = block_of(dt_of, "dt", LAG_FLOOR, LAG_DECAY, c, j)
-            acc = project(psum_vector, "vector", W_DT, c, j)
+            acc = project(psum_vector, "bank", W_DT, c, j)
             nc.vector.tensor_scalar(
                 out=dt,
                 in0=acc[:],
@@ -260,7 +269,7 @@ def tile_mamba2backbone_pb_t_kernel(
 
         def tanh_b(c, j):
             b = block_of(b_of, "b", LAG_TANH_B, LAG_SUM, c, j)
-            acc = project(psum_scalar, "scalar", W_B, c, j)
+            acc = project(psum_scalar, "bank", W_B, c, j)
             nc.scalar.activation(out=b, in_=acc[:], func=FUNC.Tanh, bias=params[:, V_B_B, j : j + 1])
 
         def finish_dt(c, pair):
@@ -276,8 +285,8 @@ def tile_mamba2backbone_pb_t_kernel(
 
         def state_terms(c, j):
             deter_term, x_term = old_block(decay_of, c, j), old_block(b_of, c, j)
-            acc = project(psum_vector, "vector", W_C, c, j)
-            turned = psum_turned.tile([P, 2, CHUNK], BF16, tag="turned")
+            acc = project(psum_vector, "bank", W_C, c, j)
+            turned = psum_turned.tile([P, 2, CHUNK], BF16, tag="bank")
             for side, source in enumerate((x_sb, deter_sb)):
                 for t in range(QUARTERS):
                     nc.tensor.transpose(
@@ -308,7 +317,7 @@ def tile_mamba2backbone_pb_t_kernel(
 
         def tanh_z(c, j):
             gate = block_of(gate_of, "gate", LAG_TANH_Z, LAG_BACK + QUARTERS - 1, c, j)
-            acc = project(psum_scalar, "scalar", W_Z, c, j)
+            acc = project(psum_scalar, "bank", W_Z, c, j)
             nc.scalar.activation(
                 out=gate, in_=acc[:], func=FUNC.Tanh, scale=0.5, bias=z_b_half[:, j : j + 1]
             )
@@ -321,7 +330,7 @@ def tile_mamba2backbone_pb_t_kernel(
                 )
 
         def back_to_rows(c, t):
-            back = psum_scalar.tile([P, CHANNELS], F32, tag="scalar")
+            back = psum_scalar.tile([P, CHANNELS], F32, tag="bank")
             back_of[(c, t)] = back
             nc.tensor.matmul(
                 out=back[:], lhsT=twice_ident[:], rhs=deter_sb[:, c * QUARTERS + t, :], start=True, stop=False

@@ -1,3 +1,4 @@
+import math
 from contextlib import ExitStack
 
 import concourse.mybir as mybir
@@ -26,7 +27,7 @@ WORDS = CHANNELS // 2
 
 DT_MIN = 1e-4
 EPS = 1e-4
-SOFTPLUS_FLOOR = -40.0
+SOFTPLUS_CAP = 40.0
 
 W_DT, W_B, W_C, W_Z = 0, 1, 2, 3
 V_DT_B, V_B_B, V_C_B, V_Z_B, V_A_BASE, V_SKIP = 0, 1, 2, 3, 4, 5
@@ -38,16 +39,16 @@ LAG_FLOOR = -1
 LAG_EXP = 0
 LAG_TANH_B = 2
 LAG_DT = 3
+LAG_DT_B = 4
 LAG_DECAY = 5
 LAG_TERMS = 6
+LAG_TANH_Z = 6
 LAG_SUM = 7
-LAG_TANH_Z = 7
-LAG_GATE = 8
 LAG_BACK = 12
 LAG_NORM = 13
 assert LAG_FLOOR - LAG_QUANTISE >= QUARTERS - 1
 assert LAG_DT + 1 - LAG_EXP >= BLOCKS
-assert LAG_BACK - LAG_GATE >= BLOCKS
+assert LAG_BACK - LAG_SUM >= BLOCKS
 
 FLOPS = 2 * TOKENS * CHANNELS * CHANNELS * 4
 
@@ -153,11 +154,11 @@ def tile_mamba2backbone_pb_t_kernel(
         make_identity(nc, ident_bf16[:])
         nc.vector.tensor_scalar_mul(out=twice_ident[:], in0=ident_bf16[:], scalar1=2.0)
         one_col = keep.tile([P, 1], F32)
-        dt_min_col = keep.tile([P, 1], F32)
+        shift_col = keep.tile([P, 1], F32)
         minus_half_col = keep.tile([P, 1], F32)
         four_eps_col = keep.tile([P, 1], F32)
         nc.vector.memset(one_col[:], 1.0)
-        nc.vector.memset(dt_min_col[:], DT_MIN)
+        nc.vector.tensor_scalar_mul(out=shift_col[:], in0=one_col[:], scalar1=math.exp(DT_MIN))
         nc.vector.memset(minus_half_col[:], -0.5)
         nc.vector.memset(four_eps_col[:], 4.0 * EPS)
 
@@ -176,12 +177,11 @@ def tile_mamba2backbone_pb_t_kernel(
             )
             nc.vector.tensor_scalar_add(out=dt_b_shifted[:], in0=params[:, V_DT_B, :], scalar1=DT_MIN)
             nc.vector.tensor_scalar_mul(out=z_b_half[:], in0=params[:, V_Z_B, :], scalar1=0.5)
-            nc.vector.tensor_scalar_max(out=a_floor[:], in0=params[:, V_A_BASE, :], scalar1=SOFTPLUS_FLOOR)
-            nc.scalar.activation(out=a_log[:], in_=a_floor[:], func=FUNC.Exp, scale=-1.0)
+            nc.vector.tensor_scalar_min(out=a_floor[:], in0=params[:, V_A_BASE, :], scalar1=SOFTPLUS_CAP)
+            nc.scalar.activation(out=a_log[:], in_=a_floor[:], func=FUNC.Exp)
 
         grouped_of = {}
         dt_of = {}
-        log_of = {}
         b_of = {}
         decay_of = {}
         gate_of = {}
@@ -245,27 +245,24 @@ def tile_mamba2backbone_pb_t_kernel(
             nc.vector.tensor_scalar(
                 out=dt,
                 in0=acc[:],
-                scalar1=dt_b_shifted[:, j : j + 1],
-                scalar2=SOFTPLUS_FLOOR,
+                scalar1=params[:, V_DT_B, j : j + 1],
+                scalar2=SOFTPLUS_CAP,
                 op0=ALU.add,
-                op1=ALU.max,
+                op1=ALU.min,
             )
 
         def exp_of_minus_m(c, j):
-            log = block_of(log_of, "log", LAG_EXP, LAG_DT, c, j)
-            nc.scalar.activation(
-                out=log, in_=old_block(dt_of, c, j), func=FUNC.Exp, scale=-1.0, bias=dt_min_col[:]
-            )
+            dt = old_block(dt_of, c, j)
+            nc.scalar.activation(out=dt, in_=dt, func=FUNC.Exp)
 
         def logs_of_chunk(c):
             if c == 0:
                 nc.scalar.activation(out=a_log[:], in_=a_log[:], func=FUNC.Ln, bias=one_col[:])
-                nc.vector.scalar_tensor_tensor(
-                    out=a_neg[:], in0=a_floor[:], scalar=-1.0, in1=a_log[:], op0=ALU.mult, op1=ALU.subtract
-                )
+                nc.vector.tensor_tensor(out=a_log[:], in0=a_log[:], in1=params[:, V_A_BASE, :], op=ALU.max)
+                nc.vector.tensor_scalar_mul(out=a_neg[:], in0=a_log[:], scalar1=-1.0)
             for pair in range(BLOCKS // 2):
-                log = whole_pair(log_of, c, pair)
-                nc.scalar.activation(out=log, in_=log, func=FUNC.Ln, bias=one_col[:])
+                log = whole_pair(dt_of, c, pair)
+                nc.scalar.activation(out=log, in_=log, func=FUNC.Ln, scale=shift_col[:], bias=shift_col[:])
 
         def tanh_b(c, j):
             b = block_of(b_of, "b", LAG_TANH_B, LAG_SUM, c, j)
@@ -273,12 +270,19 @@ def tile_mamba2backbone_pb_t_kernel(
             nc.scalar.activation(out=b, in_=acc[:], func=FUNC.Tanh, bias=params[:, V_B_B, j : j + 1])
 
         def finish_dt(c, pair):
+            for j in (2 * pair, 2 * pair + 1):
+                dt = old_block(dt_of, c, j)
+                acc = project(psum_vector, "bank", W_DT, c, j)
+                nc.vector.scalar_tensor_tensor(
+                    out=dt, in0=acc[:], scalar=dt_b_shifted[:, j : j + 1], in1=dt, op0=ALU.add, op1=ALU.max
+                )
+
+        def dt_times_b(c, pair):
             dt, b = whole_pair(dt_of, c, pair), whole_pair(b_of, c, pair)
-            nc.gpsimd.tensor_tensor(out=dt, in0=dt, in1=whole_pair(log_of, c, pair), op=ALU.add)
             nc.gpsimd.tensor_tensor(out=b, in0=dt, in1=b, op=ALU.mult)
 
         def decay(c, j):
-            d_a = block_of(decay_of, "decay", LAG_DECAY, LAG_GATE + BLOCKS - 1, c, j)
+            d_a = block_of(decay_of, "decay", LAG_DECAY, LAG_BACK + QUARTERS - 1, c, j)
             nc.scalar.activation(
                 out=d_a, in_=old_block(dt_of, c, j), func=FUNC.Exp, scale=a_neg[:, j : j + 1]
             )
@@ -312,8 +316,9 @@ def tile_mamba2backbone_pb_t_kernel(
             )
 
         def sum_terms(c, pair):
-            s = whole_pair(decay_of, c, pair)
+            s, gate = whole_pair(decay_of, c, pair), whole_pair(gate_of, c, pair)
             nc.gpsimd.tensor_tensor(out=s, in0=s, in1=whole_pair(b_of, c, pair), op=ALU.add)
+            nc.gpsimd.tensor_tensor(out=gate, in0=gate, in1=s, op=ALU.mult)
 
         def tanh_z(c, j):
             gate = block_of(gate_of, "gate", LAG_TANH_Z, LAG_BACK + QUARTERS - 1, c, j)
@@ -322,13 +327,6 @@ def tile_mamba2backbone_pb_t_kernel(
                 out=gate, in_=acc[:], func=FUNC.Tanh, scale=0.5, bias=z_b_half[:, j : j + 1]
             )
 
-        def gate_chunk(c):
-            for pair in range(BLOCKS // 2):
-                gate = whole_pair(gate_of, c, pair)
-                nc.vector.scalar_tensor_tensor(
-                    out=gate, in0=gate, scalar=1.0, in1=whole_pair(decay_of, c, pair), op0=ALU.add, op1=ALU.mult
-                )
-
         def back_to_rows(c, t):
             back = psum_scalar.tile([P, CHANNELS], F32, tag="bank")
             back_of[(c, t)] = back
@@ -336,14 +334,15 @@ def tile_mamba2backbone_pb_t_kernel(
                 out=back[:], lhsT=twice_ident[:], rhs=deter_sb[:, c * QUARTERS + t, :], start=True, stop=False
             )
             for j in range(BLOCKS):
-                nc.tensor.matmul(
-                    out=back[:, block(j)],
-                    lhsT=old_block(gate_of, c, j)[:, block(t)],
-                    rhs=ident_f32[:],
-                    is_transpose=True,
-                    start=False,
-                    stop=(j == BLOCKS - 1),
-                )
+                for last, tiles in enumerate((decay_of, gate_of)):
+                    nc.tensor.matmul(
+                        out=back[:, block(j)],
+                        lhsT=old_block(tiles, c, j)[:, block(t)],
+                        rhs=ident_f32[:],
+                        is_transpose=True,
+                        start=False,
+                        stop=(j == BLOCKS - 1 and last == 1),
+                    )
             mean = column("mean")
             mean_of[(c, t)] = mean
             squares = work.tile([P, CHANNELS], BF16, tag="squares")
@@ -386,17 +385,17 @@ def tile_mamba2backbone_pb_t_kernel(
 
         def run_step(step):
             at(step, LAG_NORM, one_over_root)
-            at_end_of_pair(step, LAG_DT, finish_dt)
+            at_end_of_pair(step, LAG_DT_B, dt_times_b)
             at_end_of_pair(step, LAG_SUM, sum_terms)
             at(step, LAG_DECAY, decay)
             at(step, LAG_TERMS, state_terms)
             at(step, LAG_TANH_Z, tanh_z)
-            at_end_of_chunk(step, LAG_GATE, gate_chunk)
             at_end_of_chunk(step, LAG_QUANTISE, quantise_chunk)
             at(step, LAG_TANH_B, tanh_b)
             at(step, LAG_BACK, back_to_rows)
             at(step, LAG_TURN_X, turn_x)
             at(step, LAG_NORM, normalise)
+            at_end_of_pair(step, LAG_DT, finish_dt)
             at(step, LAG_FLOOR, floor_dt_input)
             at(step, LAG_EXP, exp_of_minus_m)
             at_end_of_chunk(step, LAG_EXP, logs_of_chunk)

@@ -28,6 +28,8 @@ WORDS = CHANNELS // 2
 DT_MIN = 1e-4
 EPS = 1e-4
 SOFTPLUS_CAP = 40.0
+VECTOR_CHUNKS = (7,)
+MU_CHUNKS = ()
 
 W_DT, W_B, W_C, W_Z = 0, 1, 2, 3
 V_DT_B, V_B_B, V_C_B, V_Z_B, V_A_BASE, V_SKIP = 0, 1, 2, 3, 4, 5
@@ -277,9 +279,12 @@ def tile_mamba2backbone_pb_t_kernel(
                     out=dt, in0=acc[:], scalar=dt_b_shifted[:, j : j + 1], in1=dt, op0=ALU.add, op1=ALU.max
                 )
 
+        def helper(c):
+            return nc.vector if c in VECTOR_CHUNKS else nc.gpsimd
+
         def dt_times_b(c, pair):
             dt, b = whole_pair(dt_of, c, pair), whole_pair(b_of, c, pair)
-            nc.gpsimd.tensor_tensor(out=b, in0=dt, in1=b, op=ALU.mult)
+            (nc.vector if c in MU_CHUNKS else helper(c)).tensor_tensor(out=b, in0=dt, in1=b, op=ALU.mult)
 
         def decay(c, j):
             d_a = block_of(decay_of, "decay", LAG_DECAY, LAG_BACK + QUARTERS - 1, c, j)
@@ -317,8 +322,8 @@ def tile_mamba2backbone_pb_t_kernel(
 
         def sum_terms(c, pair):
             s, gate = whole_pair(decay_of, c, pair), whole_pair(gate_of, c, pair)
-            nc.gpsimd.tensor_tensor(out=s, in0=s, in1=whole_pair(b_of, c, pair), op=ALU.add)
-            nc.gpsimd.tensor_tensor(out=gate, in0=gate, in1=s, op=ALU.mult)
+            helper(c).tensor_tensor(out=s, in0=s, in1=whole_pair(b_of, c, pair), op=ALU.add)
+            helper(c).tensor_tensor(out=gate, in0=gate, in1=s, op=ALU.mult)
 
         def tanh_z(c, j):
             gate = block_of(gate_of, "gate", LAG_TANH_Z, LAG_BACK + QUARTERS - 1, c, j)

@@ -140,7 +140,6 @@ def tile_mamba2backbone_pb_t_kernel(
                 out=vector_rows[BLOCKS * v : BLOCKS * (v + 1), :],
                 in_=vector.rearrange("(j p) -> j p", p=P),
             )
-        nc.scalar.dma_start(out=norm_w_all[:], in_=norm_w.partition_broadcast(P))
         load_weight(W_DT, dt_w_words, dt_w_scales)
         load_rows(x_sb, x_rows, 1)
         load_weight(W_B, b_w_words, b_w_scales)
@@ -151,6 +150,8 @@ def tile_mamba2backbone_pb_t_kernel(
             load_rows(deter_sb, deter_rows, c)
             if c + 3 < CHUNKS:
                 load_rows(x_sb, x_rows, c + 3)
+            if c == 1:
+                nc.sync.dma_start(out=norm_w_all[:], in_=norm_w.partition_broadcast(P))
 
         make_identity(nc, ident_f32[:])
         make_identity(nc, ident_bf16[:])

@@ -323,8 +323,9 @@ def tile_mamba2backbone_pb_t_kernel(
 
         def sum_terms(c, pair):
             s, gate = whole_pair(decay_of, c, pair), whole_pair(gate_of, c, pair)
-            helper(c).tensor_tensor(out=s, in0=s, in1=whole_pair(b_of, c, pair), op=ALU.add)
-            helper(c).tensor_tensor(out=gate, in0=gate, in1=s, op=ALU.mult)
+            late = nc.vector if (c in VECTOR_CHUNKS and pair == 1) else nc.gpsimd
+            late.tensor_tensor(out=s, in0=s, in1=whole_pair(b_of, c, pair), op=ALU.add)
+            late.tensor_tensor(out=gate, in0=gate, in1=s, op=ALU.mult)
 
         def tanh_z(c, j):
             gate = block_of(gate_of, "gate", LAG_TANH_Z, LAG_BACK + QUARTERS - 1, c, j)

@@ -134,7 +134,8 @@ def tile_mamba2backbone_pb_t_kernel(
 
         nc.vector.memset(w_planes[:].rearrange("p w n -> p (w n)").bitcast(I32), 0)
         nc.vector.memset(vector_rows[:], 0.0)
-        load_rows(x_sb, x_rows, 0)
+        for t in range(QUARTERS):
+            nc.sync.dma_start(out=x_sb[:, t, :], in_=x_rows[:, t, :])
         for v, vector in enumerate((dt_b, b_b, c_b, z_b, a_base, skip)):
             nc.scalar.dma_start(
                 out=vector_rows[BLOCKS * v : BLOCKS * (v + 1), :],

@@ -52,6 +52,9 @@ assert LAG_FLOOR - LAG_QUANTISE >= QUARTERS - 1
 assert LAG_DT + 1 - LAG_EXP >= BLOCKS
 assert LAG_BACK - LAG_SUM >= BLOCKS
 
+EARLY_CHUNKS = 5
+EARLY_FROM = 2
+
 FLOPS = 2 * TOKENS * CHANNELS * CHANNELS * 4
 
 
@@ -142,15 +145,17 @@ def tile_mamba2backbone_pb_t_kernel(
                 in_=vector.rearrange("(j p) -> j p", p=P),
             )
         load_weight(W_DT, dt_w_words, dt_w_scales)
-        load_rows(x_sb, x_rows, 1)
         load_weight(W_B, b_w_words, b_w_scales)
+        load_rows(x_sb, x_rows, 1)
         load_rows(x_sb, x_rows, 2)
-        load_weight(W_C, c_w_words, c_w_scales)
         load_weight(W_Z, z_w_words, z_w_scales)
-        for c in range(CHUNKS):
+        load_weight(W_C, c_w_words, c_w_scales)
+        load_rows(x_sb, x_rows, 3)
+        load_rows(deter_sb, deter_rows, 0)
+        for c in range(4, CHUNKS):
+            load_rows(x_sb, x_rows, c)
+        for c in range(1, CHUNKS):
             load_rows(deter_sb, deter_rows, c)
-            if c + 3 < CHUNKS:
-                load_rows(x_sb, x_rows, c + 3)
             if c == 1:
                 nc.sync.dma_start(out=norm_w_all[:], in_=norm_w.partition_broadcast(P))
 
@@ -398,10 +403,17 @@ def tile_mamba2backbone_pb_t_kernel(
             at(step, LAG_DECAY, decay)
             at(step, LAG_TERMS, state_terms)
             at(step, LAG_TANH_Z, tanh_z)
-            at_end_of_chunk(step, LAG_QUANTISE, quantise_chunk)
+            if step - LAG_QUANTISE < QUARTERS or step - LAG_QUANTISE >= (EARLY_CHUNKS + 1) * QUARTERS:
+                at_end_of_chunk(step, LAG_QUANTISE, quantise_chunk)
             at(step, LAG_TANH_B, tanh_b)
             at(step, LAG_BACK, back_to_rows)
-            at(step, LAG_TURN_X, turn_x)
+            early = step - EARLY_FROM + 1
+            if 1 <= early <= EARLY_CHUNKS:
+                for t in range(QUARTERS):
+                    turn_x(early, t)
+                quantise_chunk(early)
+            if step - LAG_TURN_X < QUARTERS or step - LAG_TURN_X >= (EARLY_CHUNKS + 1) * QUARTERS:
+                at(step, LAG_TURN_X, turn_x)
             at(step, LAG_NORM, normalise)
             at_end_of_pair(step, LAG_DT, finish_dt)
             at(step, LAG_FLOOR, floor_dt_input)

import math
from contextlib import ExitStack

import concourse.mybir as mybir
from concourse.masks import make_identity

F32 = mybir.dt.float32
BF16 = mybir.dt.bfloat16
I32 = mybir.dt.int32
U32 = mybir.dt.uint32
U8 = mybir.dt.uint8
FP8X4 = mybir.dt.float8_e4m3fn_x4
ALU = mybir.AluOpType
FUNC = mybir.ActivationFunctionType

P = 128
TOKENS = 4096
CHANNELS = 512
BLOCKS = CHANNELS // P
TILES = TOKENS // P
CHUNK = 512
CHUNKS = TOKENS // CHUNK
QUARTERS = CHUNK // P
assert QUARTERS == BLOCKS
UNITS = CHUNKS * QUARTERS
WORDS = CHANNELS // 2

DT_MIN = 1e-4
EPS = 1e-4
SOFTPLUS_CAP = 40.0
VECTOR_CHUNKS = (7,)
MU_CHUNKS = ()

W_DT, W_B, W_C, W_Z = 0, 1, 2, 3
V_DT_B, V_B_B, V_C_B, V_Z_B, V_A_BASE, V_SKIP = 0, 1, 2, 3, 4, 5
VECTORS = 6

LAG_TURN_X = -5
LAG_QUANTISE = -4
LAG_FLOOR = -1
LAG_EXP = 0
LAG_TANH_B = 2
LAG_DT = 3
LAG_DT_B = 4
LAG_DECAY = 5
LAG_TERMS = 6
LAG_TANH_Z = 6
LAG_SUM = 7
LAG_BACK = 12
LAG_NORM = 13
assert LAG_FLOOR - LAG_QUANTISE >= QUARTERS - 1
assert LAG_DT + 1 - LAG_EXP >= BLOCKS
assert LAG_BACK - LAG_SUM >= BLOCKS

EARLY_CHUNKS = 5
EARLY_FROM = 2

FLOPS = 2 * TOKENS * CHANNELS * CHANNELS * 4


def pair_slots(first_lag, last_lag):
    return (last_lag - first_lag + 1) // 2 + 2


def tile_mamba2backbone_pb_t_kernel(
    tc,
    x,
    deter,
    a_base,
    dt_w_words,
    dt_w_scales,
    dt_b,
    b_w_words,
    b_w_scales,
    b_b,
    c_w_words,
    c_w_scales,
    c_b,
    z_w_words,
    z_w_scales,
    z_b,
    skip,
    norm_w,
    out,
):
    nc = tc.nc
    with ExitStack() as ctx:
        ctx.enter_context(
            tc.manual_schedule(
                engines={
                    mybir.EngineType.Activation,
                    mybir.EngineType.DVE,
                    mybir.EngineType.Pool,
                    mybir.EngineType.SP,
                }
            )
        )
        keep = ctx.enter_context(tc.tile_pool(name="keep", bufs=1))
        work = ctx.enter_context(tc.tile_pool(name="work", bufs=2))
        psum_scalar = ctx.enter_context(tc.psum_pool(name="psum", bufs=8))
        psum_vector = psum_scalar
        psum_turned = psum_scalar

        x_rows = x.rearrange("(p n) c -> p n c", n=TILES)
        deter_rows = deter.rearrange("(p n) c -> p n c", n=TILES)
        out_rows = out.rearrange("(p n) c -> p n c", n=TILES)

        x_sb = keep.tile([P, TILES, CHANNELS], BF16)
        deter_sb = keep.tile([P, TILES, CHANNELS], BF16)
        w_codes = keep.tile([P, 4, CHANNELS], U32, align_bytes=64)
        w_planes = keep.tile([P, 4, CHANNELS], U8, align_bytes=64)
        x_codes = keep.tile([P, CHUNKS, CHUNK], U32, align_bytes=64)
        x_planes = keep.tile([P, CHUNKS, CHUNK], U8, align_bytes=64)
        vector_rows = keep.tile([P, P], BF16)
        norm_w_all = keep.tile([P, CHANNELS], BF16)
        ident_bf16 = keep.tile([P, P], BF16)
        twice_ident = keep.tile([P, P], BF16)
        ident_f32 = keep.tile([P, P], F32)

        def block(j):
            return slice(j * P, (j + 1) * P)

        def load_rows(dst, src, c):
            tiles = slice(c * QUARTERS, (c + 1) * QUARTERS)
            nc.sync.dma_start(out=dst[:, tiles, :], in_=src[:, tiles, :])

        def load_weight(w, words, scales):
            for quadrant in range(4):
                nc.sync.dma_start(
                    out=w_planes[32 * quadrant : 32 * quadrant + 4, w, :].bitcast(I32),
                    in_=scales[0, 4 * quadrant : 4 * quadrant + 4, :].bitcast(I32),
                )
            nc.sync.dma_start(
                out=w_codes[:, w, :].bitcast(I32),
                in_=words[0].rearrange("p n t -> p (n t)").bitcast(I32),
            )

        nc.vector.memset(w_planes[:].rearrange("p w n -> p (w n)").bitcast(I32), 0)
        nc.vector.memset(vector_rows[:], 0.0)
        for t in range(QUARTERS):
            nc.sync.dma_start(out=x_sb[:, t, :], in_=x_rows[:, t, :])
        for v, vector in enumerate((dt_b, b_b, c_b, z_b, a_base, skip)):
            nc.scalar.dma_start(
                out=vector_rows[BLOCKS * v : BLOCKS * (v + 1), :],
                in_=vector.rearrange("(j p) -> j p", p=P),
            )
        load_weight(W_DT, dt_w_words, dt_w_scales)
        load_weight(W_B, b_w_words, b_w_scales)
        load_rows(x_sb, x_rows, 1)
        load_rows(x_sb, x_rows, 2)
        load_weight(W_Z, z_w_words, z_w_scales)
        load_weight(W_C, c_w_words, c_w_scales)
        load_rows(x_sb, x_rows, 3)
        load_rows(deter_sb, deter_rows, 0)
        for c in range(4, CHUNKS):
            load_rows(x_sb, x_rows, c)
        for c in range(1, CHUNKS):
            load_rows(deter_sb, deter_rows, c)
            if c == 1:
                nc.sync.dma_start(out=norm_w_all[:], in_=norm_w.partition_broadcast(P))

        make_identity(nc, ident_f32[:])
        make_identity(nc, ident_bf16[:])
        nc.vector.tensor_scalar_mul(out=twice_ident[:], in0=ident_bf16[:], scalar1=2.0)
        one_col = keep.tile([P, 1], F32)
        shift_col = keep.tile([P, 1], F32)
        minus_half_col = keep.tile([P, 1], F32)
        four_eps_col = keep.tile([P, 1], F32)
        nc.vector.memset(one_col[:], 1.0)
        nc.vector.tensor_scalar_mul(out=shift_col[:], in0=one_col[:], scalar1=math.exp(DT_MIN))
        nc.vector.memset(minus_half_col[:], -0.5)
        nc.vector.memset(four_eps_col[:], 4.0 * EPS)

        params = keep.tile([P, VECTORS, BLOCKS], F32)
        dt_b_shifted = keep.tile([P, BLOCKS], F32)
        z_b_half = keep.tile([P, BLOCKS], F32)
        a_floor = keep.tile([P, BLOCKS], F32)
        a_log = keep.tile([P, BLOCKS], F32)
        a_neg = keep.tile([P, BLOCKS], F32)

        def prepare_parameters():
            vectors_turned = psum_scalar.tile([P, P], BF16, tag="bank")
            nc.tensor.transpose(vectors_turned[:], vector_rows[:], ident_bf16[:])
            nc.vector.tensor_copy(
                out=params[:].rearrange("p v j -> p (v j)"), in_=vectors_turned[:, 0 : VECTORS * BLOCKS]
            )
            nc.vector.tensor_scalar_add(out=dt_b_shifted[:], in0=params[:, V_DT_B, :], scalar1=DT_MIN)
            nc.vector.tensor_scalar_mul(out=z_b_half[:], in0=params[:, V_Z_B, :], scalar1=0.5)
            nc.vector.tensor_scalar_min(out=a_floor[:], in0=params[:, V_A_BASE, :], scalar1=SOFTPLUS_CAP)
            nc.scalar.activation(out=a_log[:], in_=a_floor[:], func=FUNC.Exp)

        grouped_of = {}
        dt_of = {}
        b_of = {}
        decay_of = {}
        gate_of = {}
        back_of = {}
        mean_of = {}
        rstd_of = {}

        def block_of(tiles, tag, first_lag, last_lag, c, j):
            if j % 2 == 0:
                fresh = work.tile([P, 2, CHUNK], F32, tag=tag, bufs=pair_slots(first_lag, last_lag))
                tiles[(c, j // 2)] = fresh
            return tiles[(c, j // 2)][:, j % 2, :]

        def old_block(tiles, c, j):
            return tiles[(c, j // 2)][:, j % 2, :]

        def whole_pair(tiles, c, pair):
            return tiles[(c, pair)][:].rearrange("p h n -> p (h n)")

        def column(tag):
            fresh = work.tile([P, 1], F32, tag=tag, bufs=4)
            return fresh

        def project(pool, tag, w, c, j):
            acc = pool.tile([P, CHUNK], F32, tag=tag)
            nc.tensor.matmul_mx(
                out=acc[:],
                lhsT=w_codes[:, w, block(j)].bitcast(FP8X4),
                lhsT_scale=w_planes[:, w, block(j)],
                rhs=x_codes[:, c, :].bitcast(FP8X4),
                rhs_scale=x_planes[:, c, :],
                start=True,
                stop=True,
            )
            return acc

        def turn_x(c, t):
            if t == 0:
                fresh = work.tile([P, CHUNK, 4], BF16, tag="grouped", align_bytes=64)
                grouped_of[c] = fresh
            grouped = grouped_of[c][:, block(t), :]
            words = x_sb[:, c * QUARTERS + t, :].bitcast(F32)
            turned = psum_turned.tile([P, 2, P], F32, tag="bank")
            for u in range(2):
                nc.tensor.transpose(turned[:, u, :], words[:, u:WORDS:2], ident_f32[:])
            nc.vector.tensor_copy(
                out=grouped.rearrange("p r t -> p (r t)").bitcast(F32).rearrange("p (r u) -> p r u", u=2),
                in_=turned[:].rearrange("p u r -> p r u"),
            )

        def quantise_chunk(c):
            nc.vector.quantize_mx(
                out=x_codes[:, c, :].bitcast(FP8X4),
                scales=x_planes[:, c, :],
                in_=grouped_of[c][:].rearrange("p r t -> p (r t)"),
            )

        def floor_dt_input(c, j):
            dt = block_of(dt_of, "dt", LAG_FLOOR, LAG_DECAY, c, j)
            acc = project(psum_vector, "bank", W_DT, c, j)
            nc.vector.tensor_scalar(
                out=dt,
                in0=acc[:],
                scalar1=params[:, V_DT_B, j : j + 1],
                scalar2=SOFTPLUS_CAP,
                op0=ALU.add,
                op1=ALU.min,
            )

        def exp_of_minus_m(c, j):
            dt = old_block(dt_of, c, j)
            nc.scalar.activation(out=dt, in_=dt, func=FUNC.Exp)

        def logs_of_chunk(c):
            if c == 0:
                nc.scalar.activation(out=a_log[:], in_=a_log[:], func=FUNC.Ln, bias=one_col[:])
                nc.vector.tensor_tensor(out=a_log[:], in0=a_log[:], in1=params[:, V_A_BASE, :], op=ALU.max)
                nc.vector.tensor_scalar_mul(out=a_neg[:], in0=a_log[:], scalar1=-1.0)
            for pair in range(BLOCKS // 2):
                log = whole_pair(dt_of, c, pair)
                nc.scalar.activation(out=log, in_=log, func=FUNC.Ln, scale=shift_col[:], bias=shift_col[:])

        def tanh_b(c, j):
            b = block_of(b_of, "b", LAG_TANH_B, LAG_SUM, c, j)
            acc = project(psum_scalar, "bank", W_B, c, j)
            nc.scalar.activation(out=b, in_=acc[:], func=FUNC.Tanh, bias=params[:, V_B_B, j : j + 1])

        def finish_dt(c, pair):
            for j in (2 * pair, 2 * pair + 1):
                dt = old_block(dt_of, c, j)
                acc = project(psum_vector, "bank", W_DT, c, j)
                nc.vector.scalar_tensor_tensor(
                    out=dt, in0=acc[:], scalar=dt_b_shifted[:, j : j + 1], in1=dt, op0=ALU.add, op1=ALU.max
                )

        def helper(c):
            return nc.vector if c in VECTOR_CHUNKS else nc.gpsimd

        def dt_times_b(c, pair):
            dt, b = whole_pair(dt_of, c, pair), whole_pair(b_of, c, pair)
            (nc.vector if c in MU_CHUNKS else helper(c)).tensor_tensor(out=b, in0=dt, in1=b, op=ALU.mult)

        def decay(c, j):
            d_a = block_of(decay_of, "decay", LAG_DECAY, LAG_BACK + QUARTERS - 1, c, j)
            nc.scalar.activation(
                out=d_a, in_=old_block(dt_of, c, j), func=FUNC.Exp, scale=a_neg[:, j : j + 1]
            )

        def state_terms(c, j):
            deter_term, x_term = old_block(decay_of, c, j), old_block(b_of, c, j)
            acc = project(psum_vector, "bank", W_C, c, j)
            turned = psum_turned.tile([P, 2, CHUNK], BF16, tag="bank")
            for side, source in enumerate((x_sb, deter_sb)):
                for t in range(QUARTERS):
                    nc.tensor.transpose(
                        turned[:, side, block(t)], source[:, c * QUARTERS + t, block(j)], ident_bf16[:]
                    )
            c_bias = params[:, V_C_B, j : j + 1]
            nc.vector.scalar_tensor_tensor(
                out=deter_term, in0=acc[:], scalar=c_bias, in1=deter_term, op0=ALU.add, op1=ALU.mult
            )
            nc.vector.scalar_tensor_tensor(
                out=x_term, in0=acc[:], scalar=c_bias, in1=x_term, op0=ALU.add, op1=ALU.mult
            )
            nc.vector.scalar_tensor_tensor(
                out=deter_term, in0=deter_term, scalar=-1.0, in1=turned[:, 1, :], op0=ALU.add, op1=ALU.mult
            )
            nc.vector.scalar_tensor_tensor(
                out=x_term,
                in0=x_term,
                scalar=params[:, V_SKIP, j : j + 1],
                in1=turned[:, 0, :],
                op0=ALU.add,
                op1=ALU.mult,
            )

        def sum_terms(c, pair):
            s, gate = whole_pair(decay_of, c, pair), whole_pair(gate_of, c, pair)
            late = nc.vector if (c in VECTOR_CHUNKS and pair == 1) else nc.gpsimd
            late.tensor_tensor(out=s, in0=s, in1=whole_pair(b_of, c, pair), op=ALU.add)
            late.tensor_tensor(out=gate, in0=gate, in1=s, op=ALU.mult)

        def tanh_z(c, j):
            gate = block_of(gate_of, "gate", LAG_TANH_Z, LAG_BACK + QUARTERS - 1, c, j)
            acc = project(psum_scalar, "bank", W_Z, c, j)
            nc.scalar.activation(
                out=gate, in_=acc[:], func=FUNC.Tanh, scale=0.5, bias=z_b_half[:, j : j + 1]
            )

        def back_to_rows(c, t):
            back = psum_scalar.tile([P, CHANNELS], F32, tag="bank")
            back_of[(c, t)] = back
            nc.tensor.matmul(
                out=back[:], lhsT=twice_ident[:], rhs=deter_sb[:, c * QUARTERS + t, :], start=True, stop=False
            )
            for j in range(BLOCKS):
                for last, tiles in enumerate((decay_of, gate_of)):
                    nc.tensor.matmul(
                        out=back[:, block(j)],
                        lhsT=old_block(tiles, c, j)[:, block(t)],
                        rhs=ident_f32[:],
                        is_transpose=True,
                        start=False,
                        stop=(j == BLOCKS - 1 and last == 1),
                    )
            mean = column("mean")
            mean_of[(c, t)] = mean
            squares = work.tile([P, CHANNELS], BF16, tag="squares")
            nc.scalar.activation(
                out=squares[:], in_=back[:], func=FUNC.Square, scale=CHANNELS**-0.5, accum_out=mean[:]
            )
            nc.scalar.activation(out=mean[:], in_=mean[:], func=FUNC.Identity, bias=four_eps_col[:])

        def one_over_root(c, t):
            rstd = column("rstd")
            rstd_of[(c, t)] = rstd
            nc.gpsimd.tensor_tensor(out=rstd[:], in0=mean_of[(c, t)][:], in1=minus_half_col[:], op=ALU.pow)

        def normalise(c, t):
            result = work.tile([P, CHANNELS], F32, tag="result", bufs=4)
            nc.vector.scalar_tensor_tensor(
                out=result[:],
                in0=back_of[(c, t)][:],
                scalar=rstd_of[(c, t)][:],
                in1=norm_w_all[:],
                op0=ALU.mult,
                op1=ALU.mult,
            )
            nc.sync.dma_start(out=out_rows[:, c * QUARTERS + t, :], in_=result[:])

        def at(step, lag, stage):
            unit = step - lag
            if 0 <= unit < UNITS:
                stage(unit // QUARTERS, unit % QUARTERS)

        def at_end_of_pair(step, lag, stage):
            unit = step - lag
            if 0 <= unit < UNITS and unit % 2 == 1:
                stage(unit // QUARTERS, unit % QUARTERS // 2)

        def at_end_of_chunk(step, lag, stage):
            unit = step - lag
            if 0 <= unit < UNITS and unit % QUARTERS == QUARTERS - 1:
                stage(unit // QUARTERS)

        def run_step(step):
            at(step, LAG_NORM, one_over_root)
            at_end_of_pair(step, LAG_DT_B, dt_times_b)
            at_end_of_pair(step, LAG_SUM, sum_terms)
            at(step, LAG_DECAY, decay)
            at(step, LAG_TERMS, state_terms)
            at(step, LAG_TANH_Z, tanh_z)
            if step - LAG_QUANTISE < QUARTERS or step - LAG_QUANTISE >= (EARLY_CHUNKS + 1) * QUARTERS:
                at_end_of_chunk(step, LAG_QUANTISE, quantise_chunk)
            at(step, LAG_TANH_B, tanh_b)
            at(step, LAG_BACK, back_to_rows)
            early = step - EARLY_FROM + 1
            if 1 <= early <= EARLY_CHUNKS:
                for t in range(QUARTERS):
                    turn_x(early, t)
                quantise_chunk(early)
            if step - LAG_TURN_X < QUARTERS or step - LAG_TURN_X >= (EARLY_CHUNKS + 1) * QUARTERS:
                at(step, LAG_TURN_X, turn_x)
            at(step, LAG_NORM, normalise)
            at_end_of_pair(step, LAG_DT, finish_dt)
            at(step, LAG_FLOOR, floor_dt_input)
            at(step, LAG_EXP, exp_of_minus_m)
            at_end_of_chunk(step, LAG_EXP, logs_of_chunk)

        for step in range(LAG_TURN_X, LAG_FLOOR):
            run_step(step)
        prepare_parameters()
        for step in range(LAG_FLOOR, UNITS + LAG_NORM):
            run_step(step)
